import numpy as np
import ml_dtypes


def mxq(x, axis, fmt="e4m3"):
    dtype, down = {"e4m3": (ml_dtypes.float8_e4m3fn, 7), "e5m2": (ml_dtypes.float8_e5m2, 14)}[fmt]
    v = np.moveaxis(np.asarray(x, np.float32).astype(ml_dtypes.bfloat16).astype(np.float64), axis, -1)
    blocks = v.reshape(v.shape[:-1] + (-1, 32))
    amax = np.abs(blocks).max(-1, keepdims=True)
    byte = np.maximum(np.where(amax > 0, np.frexp(amax)[1] - 1 + 127, 0) - down, 1)
    scale = np.exp2(byte - 127.0)
    codes = (blocks / scale).astype(np.float32).astype(dtype).astype(np.float64)
    return np.moveaxis((codes * scale).reshape(v.shape), -1, axis)


WIDE = False


def mx_kscale(k):
    if not WIDE:
        return np.ones(k)
    levels = np.array([10, -10, 5, -5, 0])
    if k % 512:
        return np.exp2(np.random.permutation(np.resize(levels, k // 32))).repeat(32)
    a = np.empty((k // 512, 16))
    for p in range(k // 512):
        a[p, :8] = np.random.permutation(np.resize(levels, 8))
        for g in range(8):
            far = levels[np.abs(levels - a[p, g]) >= 10]
            a[p, g + 8] = far[np.random.randint(len(far))]
    return np.exp2(a.ravel()).repeat(32)


BF16 = ml_dtypes.bfloat16


def bf(x):
    return np.asarray(x, np.float32).astype(BF16)


def f64(x):
    return np.asarray(x).astype(np.float64)


B, H, FEAT, AUX, NS, FC, C = 1024, 1024, 128, 128, 2, 1024, 256
IN = FEAT + AUX + NS


def sigmoid(v):
    return 1.0 / (1.0 + np.exp(-v))


def draw0():
    s = mx_kscale(H)
    s = s / s.max()
    col = np.concatenate([np.full(FEAT, 0.6 / np.sqrt(FEAT)), np.full(AUX, 0.6 / np.sqrt(AUX)), np.full(NS, 0.6 / np.sqrt(NS))])
    return {"x": bf(np.random.standard_normal((B, NS))),
            "feat": bf(np.random.standard_normal((B, FEAT))),
            "aux1": bf(np.random.standard_normal((B, AUX))),
            "h": bf(np.random.standard_normal((B, H)) * s),
            "w_ih": bf(np.random.standard_normal((3 * H, IN)) * col),
            "w_hh": bf(np.random.standard_normal((3 * H, H)) / np.sqrt(H) / s),
            "b_ih": bf(np.random.standard_normal(3 * H) * 0.3),
            "b_hh": bf(np.random.standard_normal(3 * H) * 0.3)}


def core(x, feat, aux1, h, w_ih, w_hh, b_ih, b_hh):
    hh, wi, xx = f64(h), f64(w_ih), f64(x)
    gi = f64(feat) @ wi[:, :FEAT].T + f64(aux1) @ wi[:, FEAT:FEAT + AUX].T
    for j in range(NS):
        gi = gi + xx[:, j:j + 1] * wi[:, FEAT + AUX + j][None, :]
    gi = gi + f64(b_ih)
    gh = (mxq(hh, 1, "e4m3") @ mxq(f64(w_hh), 1, "e4m3").T) + f64(b_hh)
    i_r, i_z, i_n = np.split(gi, 3, axis=1)
    h_r, h_z, h_n = np.split(gh, 3, axis=1)
    r = sigmoid(i_r + h_r)
    z = sigmoid(i_z + h_z)
    n = np.tanh(i_n + r * h_n)
    return (1.0 - z) * n + z * hh


def e4m3fn_bytes(y):
    return np.clip(np.asarray(y, np.float64), -448.0, 448.0).astype(np.float32).astype(ml_dtypes.float8_e4m3fn).view(np.uint8)


def e4m3fn_values(b):
    return np.asarray(b, np.uint8).view(ml_dtypes.float8_e4m3fn).astype(np.float64)


def setup_inputs():
    d = draw0()
    x0 = np.asarray(d['w_hh']).astype(np.float64)
    s = (np.max(np.abs(x0), axis=(0,), keepdims=True) / 448.0).astype(np.float32)
    out = {}
    for k, v in d.items():
        if k == 'w_hh':
            out['w_hh_bytes'] = e4m3fn_bytes(x0 / s.astype(np.float64))
            out['w_hh_scale'] = s
        else:
            out[k] = v
    return out


def reference(x, feat, aux1, h, w_ih, w_hh_bytes, w_hh_scale, b_ih, b_hh):
    return core(x, feat, aux1, h, w_ih, e4m3fn_values(w_hh_bytes) * w_hh_scale.astype(np.float64), b_ih, b_hh)

@@ -1,0 +1,514 @@
+from contextlib import ExitStack
+
+import concourse.masks as masks
+import concourse.mybir as mybir
+
+B, H, FEAT, AUX, NS = 1024, 1024, 128, 128, 2
+IN = FEAT + AUX + NS
+FLOPS = 2 * B * H * 3 * H + 2 * B * IN * 3 * H
+
+F32 = mybir.dt.float32
+BF16 = mybir.dt.bfloat16
+U32 = mybir.dt.uint32
+U8 = mybir.dt.uint8
+FP8 = mybir.dt.float8_e4m3fn
+FP8X4 = mybir.dt.float8_e4m3fn_x4
+ALU = mybir.AluOpType
+ACT = mybir.ActivationFunctionType
+
+P = 128
+NB = 512
+SETS = 8
+UNITS = 2 * SETS
+NAMES = ("r", "z", "n")
+
+HELPED = (2, 4, 6, 8, 10, 12, 14)
+TURN_LAG = 1
+QUANT_LAG = 1
+SCALE_LAG = 1
+CAST_SHIFT = -3
+PLAIN_LEAD = 6
+HT_LEAD = 2
+O_LAG = 2
+V_TAIL = 1
+PE_JOIN = True
+J_ON_V = ((15, 0), (15, 1))
+E_SPLIT = 2
+Y_ON_G = ()
+O_ON_V = ()
+
+
+def tile_wavernncell_pa_kernel(tc, x, feat, aux1, h, w_ih, w_hh_bytes, w_hh_scale, b_ih, b_hh, out):
+    nc = tc.nc
+
+    with ExitStack() as ctx:
+        keep = ctx.enter_context(tc.tile_pool(name="keep", bufs=1))
+        stream = ctx.enter_context(tc.tile_pool(name="stream", bufs=3))
+        ew = ctx.enter_context(tc.tile_pool(name="ew", bufs=2))
+        acc = ctx.enter_context(tc.psum_pool(name="acc", bufs=1))
+        trp = ctx.enter_context(tc.psum_pool(name="trp", bufs=2))
+
+        hv = h.rearrange("(p j) k -> p j k", j=8)
+        wbv = w_hh_bytes.rearrange("(q c m) k -> c m q k", q=3, c=SETS, m=P)
+        wihv = w_ih.rearrange("(q c m) f -> q m c f", q=3, c=SETS, m=P)
+        outv = out.rearrange("(p j) n -> p j n", j=8)
+
+        s4 = keep.tile([P, 2, 1, 4], F32, name="s4")
+        h_sb = keep.tile([P, 8, H], BF16, name="h_sb")
+        wih_sb = [keep.tile([P, SETS, IN], BF16, name="wih_sb%d" % q) for q in range(3)]
+        wpad = keep.tile([P, 2, SETS, P], BF16, name="wpad")
+        brow = keep.tile([P, P], BF16, name="brow")
+        bcol = keep.tile([P, 48], F32, name="bcol")
+        brz = keep.tile([P, 16], F32, name="brz")
+        ident_f = keep.tile([P, P], F32, name="ident_f")
+        ident_b = keep.tile([P, P], BF16, name="ident_b")
+        warm = keep.tile([P, 2], F32, name="warm")
+        hg = keep.tile([P, 2, 4 * B], BF16, name="hg", align_bytes=64)
+        hq = keep.tile([P, 2, B], U32, name="hq", align_bytes=64)
+        hs = keep.tile([P, 2, B], U8, name="hs", align_bytes=64)
+        wq = keep.tile([P, SETS * 3 + 1, 256], U32, name="wq", align_bytes=64)
+        ws = keep.tile([P, SETS * 3 + 1, 256], U8, name="ws", align_bytes=64)
+        wg3 = [keep.tile([P, 4, H], BF16, name="wg%d" % k, align_bytes=64) for k in range(3)]
+        featT = keep.tile([P, B], BF16, name="featT")
+        auxT = keep.tile([P, B], BF16, name="auxT")
+        rhs3 = keep.tile([P, B], BF16, name="rhs3")
+        x0f = keep.tile([P, B], F32, name="x0f")
+        x1f = keep.tile([P, B], F32, name="x1f")
+
+        head_banks = []
+        banks_used = [0]
+
+        def bank(shape, dtype, name):
+            if head_banks:
+                tag = head_banks[banks_used[0] % len(head_banks)]
+                banks_used[0] += 1
+                if tag != "tr":
+                    return acc.tile(shape, dtype, name=name + tag, tag=tag)
+            return trp.tile(shape, dtype, name=name, tag="tr")
+
+        def two_in(which):
+            return nc.gpsimd if which == "g" else nc.vector
+
+        def copy_on(which, dst, src):
+            if which == "s":
+                nc.scalar.copy(out=dst, in_=src)
+            else:
+                nc.vector.tensor_copy(out=dst, in_=src)
+
+        def h_prep(jp, g, eng):
+            xt = bank([P, 2, 256], F32, "xt")
+            for jj in range(2):
+                words = h_sb[:, 2 * jp + jj, :].bitcast(F32)
+                for u in range(2):
+                    nc.tensor.transpose(xt[:, u, jj * P : (jj + 1) * P], words[:, 256 * g + u : 256 * (g + 1) : 2], ident_f[:])
+            dst = hg[:, g, 1024 * jp : 1024 * (jp + 1)].bitcast(F32).rearrange("p (c u) -> p c u", u=2)
+            copy_on(eng, dst, xt[:].rearrange("p u c -> p c u"))
+
+        def h_quant(g, nb):
+            nc.vector.quantize_mx(
+                out=hq[:, g, nb * NB : (nb + 1) * NB].bitcast(FP8X4),
+                scales=hs[:, g, nb * NB : (nb + 1) * NB],
+                in_=hg[:, g, nb * 4 * NB : (nb + 1) * 4 * NB],
+            )
+
+        hT_of = {}
+        pend = []
+
+        def hT_prep(c):
+            ph = bank([P, 8, P], BF16, "ph")
+            for j in range(8):
+                nc.tensor.transpose(ph[:, j, :], h_sb[:, j, c * P : (c + 1) * P], ident_b[:])
+            pend.append(("hT", c, ph))
+
+        def hT_out(c, ph):
+            hT = stream.tile([P, B], BF16, name="hT", tag="hT")
+            nc.scalar.copy(out=hT[:], in_=ph[:].rearrange("p j b -> p (j b)"))
+            hT_of[c] = hT
+
+        wT_of = {}
+
+        def wplain_prep(c):
+            pw = bank([P, 8, P], BF16, "pw")
+            for q in range(3):
+                nc.tensor.transpose(pw[:, 2 * q, :], wih_sb[q][:, c, 0:FEAT], ident_b[:])
+                nc.tensor.transpose(pw[:, 2 * q + 1, :], wih_sb[q][:, c, FEAT : FEAT + AUX], ident_b[:])
+            nc.tensor.transpose(pw[:, 6, :], wpad[:, 0, c, :], ident_b[:])
+            nc.tensor.transpose(pw[:, 7, :], wpad[:, 1, c, :], ident_b[:])
+            pend.append(("wT", c, pw))
+
+        def wT_out(c, pw):
+            wT = stream.tile([P, 8, P], BF16, name="wT", tag="wT", bufs=4)
+            nc.scalar.copy(out=wT[:], in_=pw[:])
+            wT_of[c] = wT
+
+        wby_of = {}
+        wbf_of = {}
+        xw_of = {}
+        wg_of = {}
+
+        def w_load(c):
+            wbytes = stream.tile([P, 3, H], U8, name="wbytes", tag="wbytes", bufs=4)
+            nc.sync.dma_start(out=wbytes[:], in_=wbv[c, :, :, :])
+            wby_of[c] = wbytes
+
+        def w_cast(c, q, eng="s"):
+            wbf = stream.tile([P, H], BF16, name="wbf", tag="wbf", bufs=6)
+            copy_on(eng, wbf[:], wby_of[c][:, q, :].bitcast(FP8))
+            wbf_of[(c, q)] = wbf
+
+        def w_turn(c, q):
+            words = wbf_of[(c, q)][:].bitcast(F32)
+            xt = bank([P, 2, 2, P], F32, "xw")
+            for g in range(2):
+                for u in range(2):
+                    nc.tensor.transpose(xt[:, g, u, :], words[:, 256 * g + u : 256 * (g + 1) : 2], ident_f[:])
+            xw_of[(c, q)] = xt
+
+        def w_scale(c, q):
+            xt = xw_of[(c, q)]
+            wg = wg3[c % 3]
+            for g in range(2):
+                nc.vector.tensor_tensor(
+                    out=wg[:, q, g * NB : (g + 1) * NB].rearrange("p (m u e) -> p m u e", u=2, e=2),
+                    in0=xt[:, g, :, :].rearrange("p u m -> p (u m)").bitcast(BF16).rearrange("p (u m e) -> p m u e", u=2, e=2),
+                    in1=s4[:, g, :, :].rearrange("p o (u e) -> p o u e", u=2).to_broadcast([P, P, 2, 2]),
+                    op=ALU.mult,
+                )
+
+        def w_quant(c, q):
+            if q == 2:
+                nc.vector.quantize_mx(
+                    out=wq[:, 3 * c : 3 * c + 4, :].rearrange("p t w -> p (t w)").bitcast(FP8X4),
+                    scales=ws[:, 3 * c : 3 * c + 4, :].rearrange("p t w -> p (t w)"),
+                    in_=wg3[c % 3][:].rearrange("p t k -> p (t k)"),
+                )
+
+        gi_of = {}
+        gh_of = {}
+
+        def mm_gi(i, q, part=None):
+            c, nb = i // 2, i % 2
+            cols = slice(nb * NB, (nb + 1) * NB)
+            wT = wT_of[c]
+            third = q == 2 or (q == 0 and i in HELPED)
+            if part != 1:
+                ps = acc.tile([P, NB], F32, name="gi" + NAMES[q], tag="gi" + NAMES[q])
+                gi_of[(i, q)] = ps
+                nc.tensor.matmul(ps[:], lhsT=wT[:, 2 * q, :], rhs=featT[:, cols], start=True, stop=False)
+            if part != 0:
+                ps = gi_of[(i, q)]
+                nc.tensor.matmul(ps[:], lhsT=wT[:, 2 * q + 1, :], rhs=auxT[:, cols], start=False, stop=not third)
+                if third:
+                    nc.tensor.matmul(ps[:], lhsT=wT[:, 6 if q == 2 else 7, :], rhs=rhs3[:, cols], start=False, stop=True)
+
+        def mm_gh(i, q):
+            c, nb = i // 2, i % 2
+            cols = slice(nb * NB, (nb + 1) * NB)
+            ps = acc.tile([P, NB], F32, name="gh" + NAMES[q], tag="gh" + NAMES[q])
+            for g in range(2):
+                nc.tensor.matmul_mx(
+                    out=ps[:],
+                    lhsT=wq[:, 3 * c + q, g * P : (g + 1) * P].bitcast(FP8X4),
+                    lhsT_scale=ws[:, 3 * c + q, g * P : (g + 1) * P],
+                    rhs=hq[:, g, cols].bitcast(FP8X4),
+                    rhs_scale=hs[:, g, cols],
+                    start=(g == 0),
+                    stop=(g == 1),
+                )
+            gh_of[(i, q)] = ps
+
+        def mm_rz(i):
+            mm_gi(i, 0)
+            mm_gh(i, 0)
+            mm_gh(i, 1)
+            mm_gi(i, 1)
+
+        def mm_n(i):
+            mm_gi(i, 2, 0)
+            mm_gh(i, 2)
+            mm_gi(i, 2, 1)
+
+        gate_of = {}
+        parts_of = {}
+
+        def stage_a(i):
+            c = i // 2
+            parts_of[i] = {}
+            if i in HELPED:
+                a = ew.tile([P, NB], F32, name="ar", tag="ar")
+                nc.scalar.activation(out=a[:], in_=gi_of[(i, 0)][:], func=ACT.Identity, bias=brz[:, c : c + 1], scale=1.0)
+                parts_of[i][0] = a
+
+        def stage_b(i):
+            c, nb = i // 2, i % 2
+            cols = slice(nb * NB, (nb + 1) * NB)
+            parts = parts_of[i]
+
+            def first(q):
+                a = ew.tile([P, NB], F32, name="a" + NAMES[q], tag="a" + NAMES[q])
+                nc.vector.scalar_tensor_tensor(
+                    out=a[:], in0=x0f[:, cols], scalar=wih_sb[q][:, c, 256:257], in1=gi_of[(i, q)][:], op0=ALU.mult, op1=ALU.add
+                )
+                parts[q] = a
+
+            def second(q):
+                cc = ew.tile([P, NB], F32, name="c" + NAMES[q], tag="c" + NAMES[q])
+                nc.vector.scalar_tensor_tensor(
+                    out=cc[:], in0=x1f[:, cols], scalar=wih_sb[q][:, c, 257:258], in1=gh_of[(i, q)][:], op0=ALU.mult, op1=ALU.add
+                )
+                parts[(q, 1)] = cc
+
+            if i in HELPED:
+                nc.vector.tensor_tensor(out=parts[0][:], in0=parts[0][:], in1=gh_of[(i, 0)][:], op=ALU.add)
+            else:
+                first(0)
+                second(0)
+            second(1)
+            first(1)
+
+        def stage_j(i, gates):
+            for q in gates:
+                if not (q == 0 and i in HELPED):
+                    two_in("v" if (i, q) in J_ON_V else "g").tensor_tensor(
+                        out=parts_of[i][q][:], in0=parts_of[i][q][:], in1=parts_of[i][(q, 1)][:], op=ALU.add
+                    )
+
+        def stage_s(i, q):
+            c = i // 2
+            gt = ew.tile([P, NB], F32, name="g" + NAMES[q], tag="g" + NAMES[q], bufs=3)
+            if q == 0 and i in HELPED:
+                nc.scalar.activation(out=gt[:], in_=parts_of[i][q][:], func=ACT.Sigmoid)
+            else:
+                nc.scalar.activation(out=gt[:], in_=parts_of[i][q][:], func=ACT.Sigmoid, bias=brz[:, 8 * q + c : 8 * q + c + 1], scale=1.0)
+            gate_of[(i, q)] = gt
+
+        an_of = {}
+
+        def stage_n(i):
+            c = i // 2
+            if i in Y_ON_G:
+                an = ew.tile([P, NB], F32, name="an", tag="an")
+                nc.scalar.activation(out=an[:], in_=gi_of[(i, 2)][:], func=ACT.Identity, bias=bcol[:, 16 + c : 17 + c], scale=1.0)
+                an_of[i] = an
+
+        def stage_e(i):
+            c = i // 2
+            qq = ew.tile([P, NB], F32, name="qq", tag="qq")
+            w = NB // E_SPLIT
+            for k in range(E_SPLIT):
+                cs = slice(k * w, (k + 1) * w)
+                nc.vector.scalar_tensor_tensor(
+                    out=qq[:, cs], in0=gh_of[(i, 2)][:, cs], scalar=bcol[:, 40 + c : 41 + c], in1=gate_of[(i, 0)][:, cs], op0=ALU.add, op1=ALU.mult
+                )
+            for k in range(E_SPLIT):
+                cs = slice(k * w, (k + 1) * w)
+                nc.vector.tensor_tensor(out=qq[:, cs], in0=qq[:, cs], in1=gi_of[(i, 2)][:, cs], op=ALU.add)
+            nn = ew.tile([P, NB], F32, name="nn", tag="nn", bufs=4)
+            nc.scalar.activation(out=nn[:], in_=qq[:], func=ACT.Tanh, bias=bcol[:, 16 + c : 17 + c], scale=1.0)
+            gate_of[(i, 2)] = nn
+
+        dd_of = {}
+
+        def stage_d(i, eng):
+            c, nb = i // 2, i % 2
+            cols = slice(nb * NB, (nb + 1) * NB)
+            dd = ew.tile([P, NB], F32, name="dd", tag="dd", bufs=3)
+            two_in(eng).tensor_tensor(out=dd[:], in0=hT_of[c][:, cols], in1=gate_of[(i, 2)][:], op=ALU.subtract)
+            dd_of[i] = dd
+
+        def stage_d2(i, eng):
+            two_in(eng).tensor_tensor(out=dd_of[i][:], in0=gate_of[(i, 1)][:], in1=dd_of[i][:], op=ALU.mult)
+
+        def stage_f(i, eng):
+            if not PE_JOIN:
+                two_in(eng).tensor_tensor(out=dd_of[i][:], in0=dd_of[i][:], in1=gate_of[(i, 2)][:], op=ALU.add)
+
+        def stage_o(i, eng):
+            c, nb = i // 2, i % 2
+            po = bank([P, 4, P], F32, "po")
+            for jj in range(4):
+                blk = slice(jj * P, (jj + 1) * P)
+                if PE_JOIN:
+                    nc.tensor.matmul(po[:, jj, :], lhsT=gate_of[(i, 2)][:, blk], rhs=ident_f[:], is_transpose=True, start=True, stop=False)
+                    nc.tensor.matmul(po[:, jj, :], lhsT=dd_of[i][:, blk], rhs=ident_f[:], is_transpose=True, start=False, stop=True)
+                else:
+                    nc.tensor.transpose(po[:, jj, :], dd_of[i][:, blk], ident_f[:])
+            pend.append(("o", i, po, eng))
+
+        def o_out(i, po, eng):
+            c, nb = i // 2, i % 2
+            osb = stream.tile([P, 4, P], F32, name="osb", tag="osb", bufs=4)
+            copy_on(eng, osb[:], po[:])
+            nc.sync.dma_start(out=outv[:, 4 * nb : 4 * nb + 4, c * P : (c + 1) * P], in_=osb[:])
+
+        def flush():
+            for it in pend:
+                if it[0] == "hT":
+                    hT_out(it[1], it[2])
+                elif it[0] == "wT":
+                    wT_out(it[1], it[2])
+                else:
+                    o_out(it[1], it[2], it[3])
+            pend.clear()
+
+        ctx.enter_context(tc.manual_schedule())
+
+        with tc.tile_pool(name="early", bufs=1) as early:
+            xb = early.tile([P, 2 * B], BF16, name="xb")
+            feat_sb = early.tile([P, 8, FEAT], BF16, name="feat_sb")
+            aux_sb = early.tile([P, 8, AUX], BF16, name="aux_sb")
+
+            nc.vector.memset(warm[:], 0.0)
+            nc.vector.memset(brow[:], 0.0)
+            masks.make_identity(nc, ident_f[:])
+            masks.make_identity(nc, ident_b[:])
+            nc.gpsimd.memset(wpad[:], 0.0)
+            for k in range(3):
+                nc.gpsimd.memset(wg3[k][:, 3, :], 0.0)
+
+            w_load(0)
+            nc.scalar.dma_start(out=s4[:].rearrange("p g o t -> p (g o) t"), in_=w_hh_scale.rearrange("o (g p t) -> p (o g) t", g=2, p=P, t=4))
+            nc.scalar.activation(out=warm[:, 1:2], in_=warm[:, 0:1], func=ACT.Sigmoid)
+            nc.sync.dma_start(out=h_sb[:, 0:2, :], in_=hv[:, 0:2, :])
+            nc.sync.dma_start(out=h_sb[:, 2:4, :], in_=hv[:, 2:4, :])
+            w_load(1)
+            nc.sync.dma_start(out=feat_sb[:].rearrange("p j f -> p (j f)"), in_=feat.rearrange("(p j) f -> p (j f)", j=8))
+            nc.sync.dma_start(out=aux_sb[:].rearrange("p j f -> p (j f)"), in_=aux1.rearrange("(p j) f -> p (j f)", j=8))
+            for q in range(3):
+                nc.sync.dma_start(out=wih_sb[q][:, 0:4, :], in_=wihv[q, :, 0:4, :])
+            nc.sync.dma_start(out=xb[:], in_=x.rearrange("b e -> (b e)").partition_broadcast(P))
+            nc.sync.dma_start(out=brow[0:24, :], in_=b_ih.rearrange("(r m) -> r m", m=P))
+            nc.sync.dma_start(out=brow[24:48, :], in_=b_hh.rearrange("(r m) -> r m", m=P))
+            nc.sync.dma_start(out=h_sb[:, 4:6, :], in_=hv[:, 4:6, :])
+            nc.sync.dma_start(out=h_sb[:, 6:8, :], in_=hv[:, 6:8, :])
+            w_load(2)
+            w_load(3)
+            for q in range(3):
+                nc.sync.dma_start(out=wih_sb[q][:, 4:8, :], in_=wihv[q, :, 4:8, :])
+
+            xv = xb[:].rearrange("q (p j e) -> q e j p", j=8, e=2)
+
+            def x_prep():
+                for e, xf in enumerate((x0f, x1f)):
+                    nc.gpsimd.tensor_scalar(
+                        out=xf[:].rearrange("q (j p) -> q j p", j=8), in0=xv[:, e, :, :], scalar1=1.0, scalar2=0.0, op0=ALU.mult, op1=ALU.add
+                    )
+                nc.gpsimd.tensor_scalar(out=rhs3[:], in0=x0f[:], scalar1=1.0, scalar2=0.0, op0=ALU.mult, op1=ALU.add)
+                nc.gpsimd.tensor_scalar(out=rhs3[32:64, :], in0=x1f[32:64, :], scalar1=1.0, scalar2=0.0, op0=ALU.mult, op1=ALU.add)
+
+            def wpad_prep(half):
+                cs = slice(4 * half, 4 * half + 4)
+                for a, q in enumerate((2, 0)):
+                    nc.gpsimd.tensor_copy(out=wpad[:, a, cs, 0:1], in_=wih_sb[q][:, cs, 256:257])
+                    nc.gpsimd.tensor_copy(out=wpad[:, a, cs, 32:33], in_=wih_sb[q][:, cs, 257:258])
+
+            def io_prep(half):
+                for src, dst in ((feat_sb, featT), (aux_sb, auxT)):
+                    pt = bank([P, 4, P], BF16, "pt")
+                    for jj in range(4):
+                        nc.tensor.transpose(pt[:, jj, :], src[:, 4 * half + jj, :], ident_b[:])
+                    nc.scalar.copy(out=dst[:, half * NB : (half + 1) * NB], in_=pt[:].rearrange("p j b -> p (j b)"))
+
+            def bias_prep():
+                pb = bank([P, P], BF16, "pb")
+                nc.tensor.transpose(pb[:], brow[:], ident_b[:])
+                nc.vector.tensor_copy(out=bcol[:], in_=pb[:, 0:48])
+                nc.vector.tensor_tensor(out=brz[:], in0=bcol[:, 0:16], in1=bcol[:, 24:40], op=ALU.add)
+
+            head_banks.extend(["tr", "tr", "ghn", "gin", "ghz", "ghr"])
+            for q in range(3):
+                w_cast(0, q, "v")
+            for q in range(3):
+                w_turn(0, q)
+            for jp in range(2):
+                for g in range(2):
+                    h_prep(jp, g, "s")
+            for q in range(3):
+                w_scale(0, q)
+            for q in range(3):
+                w_cast(1, q, "v")
+            for q in range(3):
+                w_turn(1, q)
+            io_prep(0)
+            wpad_prep(0)
+            x_prep()
+            wplain_prep(0)
+            flush()
+            wplain_prep(1)
+            flush()
+            for q in range(3):
+                w_quant(0, q)
+            h_quant(0, 0)
+            h_quant(1, 0)
+            for q in range(3):
+                w_scale(1, q)
+            bias_prep()
+            head_banks.clear()
+
+            cast_at = {}
+            for c in range(2, SETS):
+                for q in range(3):
+                    cast_at.setdefault(2 * (c - 2) + (0 if q < 2 else 1) + CAST_SHIFT, []).append((c, q))
+
+            def body(tau, after_b=None):
+                vt = tau - 1 >= UNITS - V_TAIL
+                flush()
+                if 0 <= tau < UNITS:
+                    stage_s(tau, 1)
+                for it in cast_at.get(tau, ()):
+                    if it[1] == 0 and it[0] + 2 < SETS:
+                        w_load(it[0] + 2)
+                    w_cast(it[0], it[1])
+                if 0 <= tau - 1 < UNITS:
+                    stage_d(tau - 1, "v" if vt else "g")
+                for it in cast_at.get(tau - TURN_LAG - 1, ()):
+                    w_scale(it[0], it[1])
+                if 0 <= tau + 1 < UNITS:
+                    stage_b(tau + 1)
+                if after_b is not None:
+                    after_b()
+                if 0 <= tau + 2 < UNITS:
+                    mm_rz(tau + 2)
+                    stage_a(tau + 2)
+                for it in cast_at.get(tau - TURN_LAG, ()):
+                    w_turn(it[0], it[1])
+                if 0 <= tau < UNITS:
+                    stage_e(tau)
+                if 0 <= tau + 1 < UNITS:
+                    mm_n(tau + 1)
+                    stage_n(tau + 1)
+                    stage_j(tau + 1, (0,))
+                    stage_s(tau + 1, 0)
+                if 0 <= tau - 1 < UNITS:
+                    stage_d2(tau - 1, "v" if vt else "g")
+                if 0 <= tau + 1 < UNITS:
+                    stage_j(tau + 1, (1,))
+                for it in cast_at.get(tau - TURN_LAG - 1 - QUANT_LAG, ()):
+                    w_quant(it[0], it[1])
+                if tau % 2 == 1 and 2 <= (tau + PLAIN_LEAD) // 2 < SETS:
+                    wplain_prep((tau + PLAIN_LEAD) // 2)
+                if tau % 2 == 0 and 1 <= (tau + HT_LEAD) // 2 < SETS:
+                    hT_prep((tau + HT_LEAD) // 2)
+                if 0 <= tau - 1 < UNITS:
+                    stage_o(tau - 1, "s")
+
+            def second_half():
+                h_quant(0, 1)
+                h_quant(1, 1)
+
+            body(-3)
+            body(-2)
+            head_banks.extend(["ghn", "gin"])
+            for jp in range(2, 4):
+                for g in range(2):
+                    h_prep(jp, g, "s")
+            io_prep(1)
+            head_banks.clear()
+            for q in range(3):
+                w_quant(1, q)
+            body(-1, second_half)
+            hT_prep(0)
+            wpad_prep(1)
+
+        for tau in range(0, UNITS + 4):
+            body(tau)

@@ -24,7 +24,7 @@ NAMES = ("r", "z", "n")
 
 HELPED = (2, 4, 6, 8, 10, 12, 14)
 TURN_LAG = 1
-QUANT_LAG = 1
+QUANT_LAG = 0
 SCALE_LAG = 1
 CAST_SHIFT = -3
 PLAIN_LEAD = 6
@@ -66,8 +66,8 @@ def tile_wavernncell_pa_kernel(tc, x, feat, aux1, h, w_ih, w_hh_bytes, w_hh_scal
         hg = keep.tile([P, 2, 4 * B], BF16, name="hg", align_bytes=64)
         hq = keep.tile([P, 2, B], U32, name="hq", align_bytes=64)
         hs = keep.tile([P, 2, B], U8, name="hs", align_bytes=64)
-        wq = keep.tile([P, SETS * 3 + 1, 256], U32, name="wq", align_bytes=64)
-        ws = keep.tile([P, SETS * 3 + 1, 256], U8, name="ws", align_bytes=64)
+        wq = keep.tile([P, SETS * 3, 256], U32, name="wq", align_bytes=64)
+        ws = keep.tile([P, SETS * 3, 256], U8, name="ws", align_bytes=64)
         wg3 = [keep.tile([P, 4, H], BF16, name="wg%d" % k, align_bytes=64) for k in range(3)]
         featT = keep.tile([P, B], BF16, name="featT")
         auxT = keep.tile([P, B], BF16, name="auxT")
@@ -164,23 +164,31 @@ def tile_wavernncell_pa_kernel(tc, x, feat, aux1, h, w_ih, w_hh_bytes, w_hh_scal
                     nc.tensor.transpose(xt[:, g, u, :], words[:, 256 * g + u : 256 * (g + 1) : 2], ident_f[:])
             xw_of[(c, q)] = xt
 
+        runs = [(0, 2), (2, 1)] + [(3 + 4 * k, 4) for k in range(5)] + [(23, 1)]
+        run_of = {}
+        for k, (first_tile, width) in enumerate(runs):
+            for a in range(width):
+                run_of[first_tile + a] = (k, a, first_tile, width)
+
         def w_scale(c, q):
             xt = xw_of[(c, q)]
-            wg = wg3[c % 3]
+            k, slot = run_of[3 * c + q][0:2]
+            wg = wg3[k % 3]
             for g in range(2):
                 nc.vector.tensor_tensor(
-                    out=wg[:, q, g * NB : (g + 1) * NB].rearrange("p (m u e) -> p m u e", u=2, e=2),
+                    out=wg[:, slot, g * NB : (g + 1) * NB].rearrange("p (m u e) -> p m u e", u=2, e=2),
                     in0=xt[:, g, :, :].rearrange("p u m -> p (u m)").bitcast(BF16).rearrange("p (u m e) -> p m u e", u=2, e=2),
                     in1=s4[:, g, :, :].rearrange("p o (u e) -> p o u e", u=2).to_broadcast([P, P, 2, 2]),
                     op=ALU.mult,
                 )
 
         def w_quant(c, q):
-            if q == 2:
+            k, slot, first_tile, width = run_of[3 * c + q]
+            if slot == width - 1:
                 nc.vector.quantize_mx(
-                    out=wq[:, 3 * c : 3 * c + 4, :].rearrange("p t w -> p (t w)").bitcast(FP8X4),
-                    scales=ws[:, 3 * c : 3 * c + 4, :].rearrange("p t w -> p (t w)"),
-                    in_=wg3[c % 3][:].rearrange("p t k -> p (t k)"),
+                    out=wq[:, first_tile : first_tile + width, :].rearrange("p t w -> p (t w)").bitcast(FP8X4),
+                    scales=ws[:, first_tile : first_tile + width, :].rearrange("p t w -> p (t w)"),
+                    in_=wg3[k % 3][:, 0:width, :].rearrange("p t k -> p (t k)"),
                 )
 
         gi_of = {}
@@ -192,7 +200,8 @@ def tile_wavernncell_pa_kernel(tc, x, feat, aux1, h, w_ih, w_hh_bytes, w_hh_scal
             wT = wT_of[c]
             third = q == 2 or (q == 0 and i in HELPED)
             if part != 1:
-                ps = acc.tile([P, NB], F32, name="gi" + NAMES[q], tag="gi" + NAMES[q])
+                nm = "gi" + NAMES[0 if (q == 2 and i == UNITS - 1) else q]
+                ps = acc.tile([P, NB], F32, name=nm, tag=nm)
                 gi_of[(i, q)] = ps
                 nc.tensor.matmul(ps[:], lhsT=wT[:, 2 * q, :], rhs=featT[:, cols], start=True, stop=False)
             if part != 0:
@@ -204,7 +213,8 @@ def tile_wavernncell_pa_kernel(tc, x, feat, aux1, h, w_ih, w_hh_bytes, w_hh_scal
         def mm_gh(i, q):
             c, nb = i // 2, i % 2
             cols = slice(nb * NB, (nb + 1) * NB)
-            ps = acc.tile([P, NB], F32, name="gh" + NAMES[q], tag="gh" + NAMES[q])
+            nm = "gh" + NAMES[0 if (q == 2 and i == UNITS - 1) else q]
+            ps = acc.tile([P, NB], F32, name=nm, tag=nm)
             for g in range(2):
                 nc.tensor.matmul_mx(
                     out=ps[:],
@@ -363,8 +373,6 @@ def tile_wavernncell_pa_kernel(tc, x, feat, aux1, h, w_ih, w_hh_bytes, w_hh_scal
             masks.make_identity(nc, ident_f[:])
             masks.make_identity(nc, ident_b[:])
             nc.gpsimd.memset(wpad[:], 0.0)
-            for k in range(3):
-                nc.gpsimd.memset(wg3[k][:, 3, :], 0.0)
 
             w_load(0)
             nc.scalar.dma_start(out=s4[:].rearrange("p g o t -> p (g o) t"), in_=w_hh_scale.rearrange("o (g p t) -> p (o g) t", g=2, p=P, t=4))
@@ -510,5 +518,29 @@ def tile_wavernncell_pa_kernel(tc, x, feat, aux1, h, w_ih, w_hh_bytes, w_hh_scal
             hT_prep(0)
             wpad_prep(1)
 
-        for tau in range(0, UNITS + 4):
+        for tau in range(0, UNITS - 2):
             body(tau)
+
+        last = UNITS - 1
+        flush()
+        stage_d(last - 2, "g")
+        stage_b(last)
+        stage_j(last, (0, 1))
+        mm_n(last)
+        stage_n(last)
+        stage_s(last, 0)
+        stage_e(last - 1)
+        stage_s(last - 1, 1)
+        stage_d2(last - 2, "g")
+        stage_s(last, 1)
+        stage_e(last)
+        stage_o(last - 2, "s")
+        stage_d(last - 1, "v")
+        flush()
+        stage_d(last, "v")
+        stage_d2(last - 1, "v")
+        stage_d2(last, "v")
+        stage_o(last - 1, "s")
+        flush()
+        stage_o(last, "s")
+        flush()

@@ -20,22 +20,11 @@ P = 128
 NB = 512
 SETS = 8
 UNITS = 2 * SETS
+LAST = UNITS - 1
+R, Z, N = 0, 1, 2
 NAMES = ("r", "z", "n")
 
 HELPED = (2, 4, 6, 8, 10, 12, 14)
-TURN_LAG = 1
-QUANT_LAG = 0
-SCALE_LAG = 1
-CAST_SHIFT = -3
-PLAIN_LEAD = 6
-HT_LEAD = 2
-O_LAG = 2
-V_TAIL = 1
-PE_JOIN = True
-J_ON_V = ((15, 0), (15, 1))
-E_SPLIT = 2
-Y_ON_G = ()
-O_ON_V = ()
 
 
 def tile_wavernncell_pa_kernel(tc, x, feat, aux1, h, w_ih, w_hh_bytes, w_hh_scale, b_ih, b_hh, out):
@@ -75,36 +64,29 @@ def tile_wavernncell_pa_kernel(tc, x, feat, aux1, h, w_ih, w_hh_bytes, w_hh_scal
         x0f = keep.tile([P, B], F32, name="x0f")
         x1f = keep.tile([P, B], F32, name="x1f")
 
-        head_banks = []
-        banks_used = [0]
+        spare_banks = []
+        spare_used = [0]
 
         def bank(shape, dtype, name):
-            if head_banks:
-                tag = head_banks[banks_used[0] % len(head_banks)]
-                banks_used[0] += 1
+            if spare_banks:
+                tag = spare_banks[spare_used[0] % len(spare_banks)]
+                spare_used[0] += 1
                 if tag != "tr":
                     return acc.tile(shape, dtype, name=name + tag, tag=tag)
             return trp.tile(shape, dtype, name=name, tag="tr")
 
-        def two_in(which):
-            return nc.gpsimd if which == "g" else nc.vector
+        pending = []
 
-        def copy_on(which, dst, src):
-            if which == "s":
-                nc.scalar.copy(out=dst, in_=src)
-            else:
-                nc.vector.tensor_copy(out=dst, in_=src)
-
-        def h_prep(jp, g, eng):
+        def h_turn(jp, g):
             xt = bank([P, 2, 256], F32, "xt")
             for jj in range(2):
                 words = h_sb[:, 2 * jp + jj, :].bitcast(F32)
                 for u in range(2):
                     nc.tensor.transpose(xt[:, u, jj * P : (jj + 1) * P], words[:, 256 * g + u : 256 * (g + 1) : 2], ident_f[:])
             dst = hg[:, g, 1024 * jp : 1024 * (jp + 1)].bitcast(F32).rearrange("p (c u) -> p c u", u=2)
-            copy_on(eng, dst, xt[:].rearrange("p u c -> p c u"))
+            nc.scalar.copy(out=dst, in_=xt[:].rearrange("p u c -> p c u"))
 
-        def h_quant(g, nb):
+        def h_quantize(g, nb):
             nc.vector.quantize_mx(
                 out=hq[:, g, nb * NB : (nb + 1) * NB].bitcast(FP8X4),
                 scales=hs[:, g, nb * NB : (nb + 1) * NB],
@@ -112,48 +94,49 @@ def tile_wavernncell_pa_kernel(tc, x, feat, aux1, h, w_ih, w_hh_bytes, w_hh_scal
             )
 
         hT_of = {}
-        pend = []
 
-        def hT_prep(c):
+        def hT_turn(c):
             ph = bank([P, 8, P], BF16, "ph")
             for j in range(8):
                 nc.tensor.transpose(ph[:, j, :], h_sb[:, j, c * P : (c + 1) * P], ident_b[:])
-            pend.append(("hT", c, ph))
+            pending.append(("hT", c, ph))
 
-        def hT_out(c, ph):
+        def hT_copy(c, ph):
             hT = stream.tile([P, B], BF16, name="hT", tag="hT")
             nc.scalar.copy(out=hT[:], in_=ph[:].rearrange("p j b -> p (j b)"))
             hT_of[c] = hT
 
         wT_of = {}
 
-        def wplain_prep(c):
+        def wT_turn(c):
             pw = bank([P, 8, P], BF16, "pw")
             for q in range(3):
                 nc.tensor.transpose(pw[:, 2 * q, :], wih_sb[q][:, c, 0:FEAT], ident_b[:])
                 nc.tensor.transpose(pw[:, 2 * q + 1, :], wih_sb[q][:, c, FEAT : FEAT + AUX], ident_b[:])
             nc.tensor.transpose(pw[:, 6, :], wpad[:, 0, c, :], ident_b[:])
             nc.tensor.transpose(pw[:, 7, :], wpad[:, 1, c, :], ident_b[:])
-            pend.append(("wT", c, pw))
+            pending.append(("wT", c, pw))
 
-        def wT_out(c, pw):
+        def wT_copy(c, pw):
             wT = stream.tile([P, 8, P], BF16, name="wT", tag="wT", bufs=4)
             nc.scalar.copy(out=wT[:], in_=pw[:])
             wT_of[c] = wT
 
-        wby_of = {}
+        wbytes_of = {}
         wbf_of = {}
         xw_of = {}
-        wg_of = {}
 
         def w_load(c):
             wbytes = stream.tile([P, 3, H], U8, name="wbytes", tag="wbytes", bufs=4)
             nc.sync.dma_start(out=wbytes[:], in_=wbv[c, :, :, :])
-            wby_of[c] = wbytes
+            wbytes_of[c] = wbytes
 
-        def w_cast(c, q, eng="s"):
+        def w_cast(c, q, on_vector=False):
             wbf = stream.tile([P, H], BF16, name="wbf", tag="wbf", bufs=6)
-            copy_on(eng, wbf[:], wby_of[c][:, q, :].bitcast(FP8))
+            if on_vector:
+                nc.vector.tensor_copy(out=wbf[:], in_=wbytes_of[c][:, q, :].bitcast(FP8))
+            else:
+                nc.scalar.copy(out=wbf[:], in_=wbytes_of[c][:, q, :].bitcast(FP8))
             wbf_of[(c, q)] = wbf
 
         def w_turn(c, q):
@@ -182,7 +165,7 @@ def tile_wavernncell_pa_kernel(tc, x, feat, aux1, h, w_ih, w_hh_bytes, w_hh_scal
                     op=ALU.mult,
                 )
 
-        def w_quant(c, q):
+        def w_quantize(c, q):
             k, slot, first_tile, width = run_of[3 * c + q]
             if slot == width - 1:
                 nc.vector.quantize_mx(
@@ -194,26 +177,29 @@ def tile_wavernncell_pa_kernel(tc, x, feat, aux1, h, w_ih, w_hh_bytes, w_hh_scal
         gi_of = {}
         gh_of = {}
 
-        def mm_gi(i, q, part=None):
+        def bank_name(kind, i, q):
+            return kind + NAMES[R if (q == N and i == LAST) else q]
+
+        def mm_gi(i, q, first=True, rest=True):
             c, nb = i // 2, i % 2
             cols = slice(nb * NB, (nb + 1) * NB)
             wT = wT_of[c]
-            third = q == 2 or (q == 0 and i in HELPED)
-            if part != 1:
-                nm = "gi" + NAMES[0 if (q == 2 and i == UNITS - 1) else q]
+            with_x = q == N or (q == R and i in HELPED)
+            if first:
+                nm = bank_name("gi", i, q)
                 ps = acc.tile([P, NB], F32, name=nm, tag=nm)
                 gi_of[(i, q)] = ps
                 nc.tensor.matmul(ps[:], lhsT=wT[:, 2 * q, :], rhs=featT[:, cols], start=True, stop=False)
-            if part != 0:
+            if rest:
                 ps = gi_of[(i, q)]
-                nc.tensor.matmul(ps[:], lhsT=wT[:, 2 * q + 1, :], rhs=auxT[:, cols], start=False, stop=not third)
-                if third:
-                    nc.tensor.matmul(ps[:], lhsT=wT[:, 6 if q == 2 else 7, :], rhs=rhs3[:, cols], start=False, stop=True)
+                nc.tensor.matmul(ps[:], lhsT=wT[:, 2 * q + 1, :], rhs=auxT[:, cols], start=False, stop=not with_x)
+                if with_x:
+                    nc.tensor.matmul(ps[:], lhsT=wT[:, 6 if q == N else 7, :], rhs=rhs3[:, cols], start=False, stop=True)
 
         def mm_gh(i, q):
             c, nb = i // 2, i % 2
             cols = slice(nb * NB, (nb + 1) * NB)
-            nm = "gh" + NAMES[0 if (q == 2 and i == UNITS - 1) else q]
+            nm = bank_name("gh", i, q)
             ps = acc.tile([P, NB], F32, name=nm, tag=nm)
             for g in range(2):
                 nc.tensor.matmul_mx(
@@ -228,138 +214,115 @@ def tile_wavernncell_pa_kernel(tc, x, feat, aux1, h, w_ih, w_hh_bytes, w_hh_scal
             gh_of[(i, q)] = ps
 
         def mm_rz(i):
-            mm_gi(i, 0)
-            mm_gh(i, 0)
-            mm_gh(i, 1)
-            mm_gi(i, 1)
+            mm_gi(i, R)
+            mm_gh(i, R)
+            mm_gh(i, Z)
+            mm_gi(i, Z)
 
         def mm_n(i):
-            mm_gi(i, 2, 0)
-            mm_gh(i, 2)
-            mm_gi(i, 2, 1)
+            mm_gi(i, N, rest=False)
+            mm_gh(i, N)
+            mm_gi(i, N, first=False)
 
         gate_of = {}
-        parts_of = {}
+        sum_of = {}
 
-        def stage_a(i):
+        def r_helped_copy(i):
             c = i // 2
-            parts_of[i] = {}
             if i in HELPED:
                 a = ew.tile([P, NB], F32, name="ar", tag="ar")
-                nc.scalar.activation(out=a[:], in_=gi_of[(i, 0)][:], func=ACT.Identity, bias=brz[:, c : c + 1], scale=1.0)
-                parts_of[i][0] = a
+                nc.scalar.activation(out=a[:], in_=gi_of[(i, R)][:], func=ACT.Identity, bias=brz[:, c : c + 1], scale=1.0)
+                sum_of[(i, R)] = a
 
-        def stage_b(i):
+        def rz_empty(i):
             c, nb = i // 2, i % 2
             cols = slice(nb * NB, (nb + 1) * NB)
-            parts = parts_of[i]
 
-            def first(q):
+            def gi_half(q):
                 a = ew.tile([P, NB], F32, name="a" + NAMES[q], tag="a" + NAMES[q])
                 nc.vector.scalar_tensor_tensor(
                     out=a[:], in0=x0f[:, cols], scalar=wih_sb[q][:, c, 256:257], in1=gi_of[(i, q)][:], op0=ALU.mult, op1=ALU.add
                 )
-                parts[q] = a
+                sum_of[(i, q)] = a
 
-            def second(q):
+            def gh_half(q):
                 cc = ew.tile([P, NB], F32, name="c" + NAMES[q], tag="c" + NAMES[q])
                 nc.vector.scalar_tensor_tensor(
                     out=cc[:], in0=x1f[:, cols], scalar=wih_sb[q][:, c, 257:258], in1=gh_of[(i, q)][:], op0=ALU.mult, op1=ALU.add
                 )
-                parts[(q, 1)] = cc
+                sum_of[(i, q, "h")] = cc
 
             if i in HELPED:
-                nc.vector.tensor_tensor(out=parts[0][:], in0=parts[0][:], in1=gh_of[(i, 0)][:], op=ALU.add)
+                nc.vector.tensor_tensor(out=sum_of[(i, R)][:], in0=sum_of[(i, R)][:], in1=gh_of[(i, R)][:], op=ALU.add)
             else:
-                first(0)
-                second(0)
-            second(1)
-            first(1)
+                gi_half(R)
+                gh_half(R)
+            gh_half(Z)
+            gi_half(Z)
 
-        def stage_j(i, gates):
-            for q in gates:
-                if not (q == 0 and i in HELPED):
-                    two_in("v" if (i, q) in J_ON_V else "g").tensor_tensor(
-                        out=parts_of[i][q][:], in0=parts_of[i][q][:], in1=parts_of[i][(q, 1)][:], op=ALU.add
-                    )
+        def rz_sum(i, q):
+            if not (q == R and i in HELPED):
+                engine = nc.vector if i == LAST else nc.gpsimd
+                engine.tensor_tensor(out=sum_of[(i, q)][:], in0=sum_of[(i, q)][:], in1=sum_of[(i, q, "h")][:], op=ALU.add)
 
-        def stage_s(i, q):
+        def rz_sigmoid(i, q):
             c = i // 2
             gt = ew.tile([P, NB], F32, name="g" + NAMES[q], tag="g" + NAMES[q], bufs=3)
-            if q == 0 and i in HELPED:
-                nc.scalar.activation(out=gt[:], in_=parts_of[i][q][:], func=ACT.Sigmoid)
+            if q == R and i in HELPED:
+                nc.scalar.activation(out=gt[:], in_=sum_of[(i, q)][:], func=ACT.Sigmoid)
             else:
-                nc.scalar.activation(out=gt[:], in_=parts_of[i][q][:], func=ACT.Sigmoid, bias=brz[:, 8 * q + c : 8 * q + c + 1], scale=1.0)
+                nc.scalar.activation(out=gt[:], in_=sum_of[(i, q)][:], func=ACT.Sigmoid, bias=brz[:, 8 * q + c : 8 * q + c + 1], scale=1.0)
             gate_of[(i, q)] = gt
 
-        an_of = {}
-
-        def stage_n(i):
-            c = i // 2
-            if i in Y_ON_G:
-                an = ew.tile([P, NB], F32, name="an", tag="an")
-                nc.scalar.activation(out=an[:], in_=gi_of[(i, 2)][:], func=ACT.Identity, bias=bcol[:, 16 + c : 17 + c], scale=1.0)
-                an_of[i] = an
-
-        def stage_e(i):
+        def n_gate(i):
             c = i // 2
             qq = ew.tile([P, NB], F32, name="qq", tag="qq")
-            w = NB // E_SPLIT
-            for k in range(E_SPLIT):
-                cs = slice(k * w, (k + 1) * w)
+            halves = (slice(0, NB // 2), slice(NB // 2, NB))
+            for cs in halves:
                 nc.vector.scalar_tensor_tensor(
-                    out=qq[:, cs], in0=gh_of[(i, 2)][:, cs], scalar=bcol[:, 40 + c : 41 + c], in1=gate_of[(i, 0)][:, cs], op0=ALU.add, op1=ALU.mult
+                    out=qq[:, cs], in0=gh_of[(i, N)][:, cs], scalar=bcol[:, 40 + c : 41 + c], in1=gate_of[(i, R)][:, cs], op0=ALU.add, op1=ALU.mult
                 )
-            for k in range(E_SPLIT):
-                cs = slice(k * w, (k + 1) * w)
-                nc.vector.tensor_tensor(out=qq[:, cs], in0=qq[:, cs], in1=gi_of[(i, 2)][:, cs], op=ALU.add)
+            for cs in halves:
+                nc.vector.tensor_tensor(out=qq[:, cs], in0=qq[:, cs], in1=gi_of[(i, N)][:, cs], op=ALU.add)
             nn = ew.tile([P, NB], F32, name="nn", tag="nn", bufs=4)
             nc.scalar.activation(out=nn[:], in_=qq[:], func=ACT.Tanh, bias=bcol[:, 16 + c : 17 + c], scale=1.0)
-            gate_of[(i, 2)] = nn
+            gate_of[(i, N)] = nn
 
         dd_of = {}
 
-        def stage_d(i, eng):
+        def h_minus_n(i, engine):
             c, nb = i // 2, i % 2
             cols = slice(nb * NB, (nb + 1) * NB)
             dd = ew.tile([P, NB], F32, name="dd", tag="dd", bufs=3)
-            two_in(eng).tensor_tensor(out=dd[:], in0=hT_of[c][:, cols], in1=gate_of[(i, 2)][:], op=ALU.subtract)
+            engine.tensor_tensor(out=dd[:], in0=hT_of[c][:, cols], in1=gate_of[(i, N)][:], op=ALU.subtract)
             dd_of[i] = dd
 
-        def stage_d2(i, eng):
-            two_in(eng).tensor_tensor(out=dd_of[i][:], in0=gate_of[(i, 1)][:], in1=dd_of[i][:], op=ALU.mult)
+        def times_z(i, engine):
+            engine.tensor_tensor(out=dd_of[i][:], in0=gate_of[(i, Z)][:], in1=dd_of[i][:], op=ALU.mult)
 
-        def stage_f(i, eng):
-            if not PE_JOIN:
-                two_in(eng).tensor_tensor(out=dd_of[i][:], in0=dd_of[i][:], in1=gate_of[(i, 2)][:], op=ALU.add)
-
-        def stage_o(i, eng):
-            c, nb = i // 2, i % 2
+        def out_turn(i):
             po = bank([P, 4, P], F32, "po")
             for jj in range(4):
                 blk = slice(jj * P, (jj + 1) * P)
-                if PE_JOIN:
-                    nc.tensor.matmul(po[:, jj, :], lhsT=gate_of[(i, 2)][:, blk], rhs=ident_f[:], is_transpose=True, start=True, stop=False)
-                    nc.tensor.matmul(po[:, jj, :], lhsT=dd_of[i][:, blk], rhs=ident_f[:], is_transpose=True, start=False, stop=True)
-                else:
-                    nc.tensor.transpose(po[:, jj, :], dd_of[i][:, blk], ident_f[:])
-            pend.append(("o", i, po, eng))
+                nc.tensor.matmul(po[:, jj, :], lhsT=gate_of[(i, N)][:, blk], rhs=ident_f[:], is_transpose=True, start=True, stop=False)
+                nc.tensor.matmul(po[:, jj, :], lhsT=dd_of[i][:, blk], rhs=ident_f[:], is_transpose=True, start=False, stop=True)
+            pending.append(("out", i, po))
 
-        def o_out(i, po, eng):
+        def out_store(i, po):
             c, nb = i // 2, i % 2
             osb = stream.tile([P, 4, P], F32, name="osb", tag="osb", bufs=4)
-            copy_on(eng, osb[:], po[:])
+            nc.scalar.copy(out=osb[:], in_=po[:])
             nc.sync.dma_start(out=outv[:, 4 * nb : 4 * nb + 4, c * P : (c + 1) * P], in_=osb[:])
 
-        def flush():
-            for it in pend:
-                if it[0] == "hT":
-                    hT_out(it[1], it[2])
-                elif it[0] == "wT":
-                    wT_out(it[1], it[2])
+        def copies_out():
+            for what, index, ps in pending:
+                if what == "hT":
+                    hT_copy(index, ps)
+                elif what == "wT":
+                    wT_copy(index, ps)
                 else:
-                    o_out(it[1], it[2], it[3])
-            pend.clear()
+                    out_store(index, ps)
+            pending.clear()
 
         ctx.enter_context(tc.manual_schedule())
 
@@ -396,7 +359,7 @@ def tile_wavernncell_pa_kernel(tc, x, feat, aux1, h, w_ih, w_hh_bytes, w_hh_scal
 
             xv = xb[:].rearrange("q (p j e) -> q e j p", j=8, e=2)
 
-            def x_prep():
+            def x_spread():
                 for e, xf in enumerate((x0f, x1f)):
                     nc.gpsimd.tensor_scalar(
                         out=xf[:].rearrange("q (j p) -> q j p", j=8), in0=xv[:, e, :, :], scalar1=1.0, scalar2=0.0, op0=ALU.mult, op1=ALU.add
@@ -404,143 +367,172 @@ def tile_wavernncell_pa_kernel(tc, x, feat, aux1, h, w_ih, w_hh_bytes, w_hh_scal
                 nc.gpsimd.tensor_scalar(out=rhs3[:], in0=x0f[:], scalar1=1.0, scalar2=0.0, op0=ALU.mult, op1=ALU.add)
                 nc.gpsimd.tensor_scalar(out=rhs3[32:64, :], in0=x1f[32:64, :], scalar1=1.0, scalar2=0.0, op0=ALU.mult, op1=ALU.add)
 
-            def wpad_prep(half):
+            def wpad_fill(half):
                 cs = slice(4 * half, 4 * half + 4)
-                for a, q in enumerate((2, 0)):
+                for a, q in enumerate((N, R)):
                     nc.gpsimd.tensor_copy(out=wpad[:, a, cs, 0:1], in_=wih_sb[q][:, cs, 256:257])
                     nc.gpsimd.tensor_copy(out=wpad[:, a, cs, 32:33], in_=wih_sb[q][:, cs, 257:258])
 
-            def io_prep(half):
+            def feat_aux_turn(half):
                 for src, dst in ((feat_sb, featT), (aux_sb, auxT)):
                     pt = bank([P, 4, P], BF16, "pt")
                     for jj in range(4):
                         nc.tensor.transpose(pt[:, jj, :], src[:, 4 * half + jj, :], ident_b[:])
                     nc.scalar.copy(out=dst[:, half * NB : (half + 1) * NB], in_=pt[:].rearrange("p j b -> p (j b)"))
 
-            def bias_prep():
+            def bias_turn():
                 pb = bank([P, P], BF16, "pb")
                 nc.tensor.transpose(pb[:], brow[:], ident_b[:])
                 nc.vector.tensor_copy(out=bcol[:], in_=pb[:, 0:48])
                 nc.vector.tensor_tensor(out=brz[:], in0=bcol[:, 0:16], in1=bcol[:, 24:40], op=ALU.add)
 
-            head_banks.extend(["tr", "tr", "ghn", "gin", "ghz", "ghr"])
+            spare_banks.extend(["tr", "tr", "ghn", "gin", "ghz", "ghr"])
             for q in range(3):
-                w_cast(0, q, "v")
+                w_cast(0, q, on_vector=True)
             for q in range(3):
                 w_turn(0, q)
             for jp in range(2):
                 for g in range(2):
-                    h_prep(jp, g, "s")
+                    h_turn(jp, g)
             for q in range(3):
                 w_scale(0, q)
             for q in range(3):
-                w_cast(1, q, "v")
+                w_cast(1, q, on_vector=True)
             for q in range(3):
                 w_turn(1, q)
-            io_prep(0)
-            wpad_prep(0)
-            x_prep()
-            wplain_prep(0)
-            flush()
-            wplain_prep(1)
-            flush()
+            feat_aux_turn(0)
+            wpad_fill(0)
+            x_spread()
+            wT_turn(0)
+            copies_out()
+            wT_turn(1)
+            copies_out()
             for q in range(3):
-                w_quant(0, q)
-            h_quant(0, 0)
-            h_quant(1, 0)
+                w_quantize(0, q)
+            h_quantize(0, 0)
+            h_quantize(1, 0)
             for q in range(3):
                 w_scale(1, q)
-            bias_prep()
-            head_banks.clear()
+            bias_turn()
+            spare_banks.clear()
 
-            cast_at = {}
+            cast_in = {}
             for c in range(2, SETS):
                 for q in range(3):
-                    cast_at.setdefault(2 * (c - 2) + (0 if q < 2 else 1) + CAST_SHIFT, []).append((c, q))
+                    cast_in.setdefault(2 * c - 7 + (0 if q < N else 1), []).append((c, q))
 
-            def body(tau, after_b=None):
-                vt = tau - 1 >= UNITS - V_TAIL
-                flush()
-                if 0 <= tau < UNITS:
-                    stage_s(tau, 1)
-                for it in cast_at.get(tau, ()):
-                    if it[1] == 0 and it[0] + 2 < SETS:
-                        w_load(it[0] + 2)
-                    w_cast(it[0], it[1])
-                if 0 <= tau - 1 < UNITS:
-                    stage_d(tau - 1, "v" if vt else "g")
-                for it in cast_at.get(tau - TURN_LAG - 1, ()):
-                    w_scale(it[0], it[1])
-                if 0 <= tau + 1 < UNITS:
-                    stage_b(tau + 1)
-                if after_b is not None:
-                    after_b()
-                if 0 <= tau + 2 < UNITS:
+            def is_unit(i):
+                return 0 <= i < UNITS
+
+            def step(tau, after_rz_empty=None, with_out=True):
+                copies_out()
+                if is_unit(tau):
+                    rz_sigmoid(tau, Z)
+                for c, q in cast_in.get(tau, ()):
+                    if q == R and c + 2 < SETS:
+                        w_load(c + 2)
+                    w_cast(c, q)
+                if is_unit(tau - 1):
+                    h_minus_n(tau - 1, nc.gpsimd)
+                for c, q in cast_in.get(tau - 2, ()):
+                    w_scale(c, q)
+                if is_unit(tau + 1):
+                    rz_empty(tau + 1)
+                if after_rz_empty is not None:
+                    after_rz_empty()
+                if is_unit(tau + 2):
                     mm_rz(tau + 2)
-                    stage_a(tau + 2)
-                for it in cast_at.get(tau - TURN_LAG, ()):
-                    w_turn(it[0], it[1])
-                if 0 <= tau < UNITS:
-                    stage_e(tau)
-                if 0 <= tau + 1 < UNITS:
+                    r_helped_copy(tau + 2)
+                for c, q in cast_in.get(tau - 1, ()):
+                    w_turn(c, q)
+                if is_unit(tau):
+                    n_gate(tau)
+                if is_unit(tau + 1):
                     mm_n(tau + 1)
-                    stage_n(tau + 1)
-                    stage_j(tau + 1, (0,))
-                    stage_s(tau + 1, 0)
-                if 0 <= tau - 1 < UNITS:
-                    stage_d2(tau - 1, "v" if vt else "g")
-                if 0 <= tau + 1 < UNITS:
-                    stage_j(tau + 1, (1,))
-                for it in cast_at.get(tau - TURN_LAG - 1 - QUANT_LAG, ()):
-                    w_quant(it[0], it[1])
-                if tau % 2 == 1 and 2 <= (tau + PLAIN_LEAD) // 2 < SETS:
-                    wplain_prep((tau + PLAIN_LEAD) // 2)
-                if tau % 2 == 0 and 1 <= (tau + HT_LEAD) // 2 < SETS:
-                    hT_prep((tau + HT_LEAD) // 2)
-                if 0 <= tau - 1 < UNITS:
-                    stage_o(tau - 1, "s")
+                    rz_sum(tau + 1, R)
+                    rz_sigmoid(tau + 1, R)
+                if is_unit(tau - 1):
+                    times_z(tau - 1, nc.gpsimd)
+                if is_unit(tau + 1):
+                    rz_sum(tau + 1, Z)
+                for c, q in cast_in.get(tau - 2, ()):
+                    w_quantize(c, q)
+                if tau % 2 == 1 and 2 <= (tau + 5) // 2 < SETS:
+                    wT_turn((tau + 5) // 2)
+                if tau % 2 == 0 and 1 <= (tau + 2) // 2 < SETS:
+                    hT_turn((tau + 2) // 2)
+                if is_unit(tau - 1) and with_out:
+                    out_turn(tau - 1)
 
-            def second_half():
-                h_quant(0, 1)
-                h_quant(1, 1)
+            def quantize_second_half():
+                h_quantize(0, 1)
+                h_quantize(1, 1)
 
-            body(-3)
-            body(-2)
-            head_banks.extend(["ghn", "gin"])
+            step(-3)
+            step(-2)
+            spare_banks.extend(["ghn", "gin"])
             for jp in range(2, 4):
                 for g in range(2):
-                    h_prep(jp, g, "s")
-            io_prep(1)
-            head_banks.clear()
+                    h_turn(jp, g)
+            feat_aux_turn(1)
+            spare_banks.clear()
             for q in range(3):
-                w_quant(1, q)
-            body(-1, second_half)
-            hT_prep(0)
-            wpad_prep(1)
+                w_quantize(1, q)
+            step(-1, quantize_second_half)
+            hT_turn(0)
+            wpad_fill(1)
 
-        for tau in range(0, UNITS - 2):
-            body(tau)
+        for tau in range(0, LAST - 2):
+            step(tau)
+        step(LAST - 2, with_out=False)
 
-        last = UNITS - 1
-        flush()
-        stage_d(last - 2, "g")
-        stage_b(last)
-        stage_j(last, (0, 1))
-        mm_n(last)
-        stage_n(last)
-        stage_s(last, 0)
-        stage_e(last - 1)
-        stage_s(last - 1, 1)
-        stage_d2(last - 2, "g")
-        stage_s(last, 1)
-        stage_e(last)
-        stage_o(last - 2, "s")
-        stage_d(last - 1, "v")
-        flush()
-        stage_d(last, "v")
-        stage_d2(last - 1, "v")
-        stage_d2(last, "v")
-        stage_o(last - 1, "s")
-        flush()
-        stage_o(last, "s")
-        flush()
+        copies_out()
+        h_minus_n(LAST - 2, nc.gpsimd)
+        rz_empty(LAST)
+        rz_sum(LAST, R)
+        rz_sum(LAST, Z)
+        mm_n(LAST)
+        out_turn(LAST - 3)
+        rz_sigmoid(LAST, R)
+        rz_sigmoid(LAST - 1, Z)
+        rz_sigmoid(LAST, Z)
+        n_gate(LAST - 1)
+        copies_out()
+        times_z(LAST - 2, nc.gpsimd)
+        c = LAST // 2
+        qq = ew.tile([P, NB], F32, name="qq", tag="qq")
+        nn = ew.tile([P, NB], F32, name="nn", tag="nn", bufs=4)
+        dd = ew.tile([P, NB], F32, name="dd", tag="dd", bufs=3)
+        halves = (slice(0, NB // 2), slice(NB // 2, NB))
+        for cs in halves:
+            nc.vector.scalar_tensor_tensor(
+                out=qq[:, cs], in0=gh_of[(LAST, N)][:, cs], scalar=bcol[:, 40 + c : 41 + c], in1=gate_of[(LAST, R)][:, cs], op0=ALU.add, op1=ALU.mult
+            )
+        for cs in halves:
+            nc.vector.tensor_tensor(out=qq[:, cs], in0=qq[:, cs], in1=gi_of[(LAST, N)][:, cs], op=ALU.add)
+            nc.scalar.activation(out=nn[:, cs], in_=qq[:, cs], func=ACT.Tanh, bias=bcol[:, 16 + c : 17 + c], scale=1.0)
+        spare_used[0] = 0
+        spare_banks.extend(["tr", "giz", "ghz", "gin"])
+        out_turn(LAST - 2)
+        h_minus_n(LAST - 1, nc.vector)
+        copies_out()
+        hT_last = hT_of[c][:, NB : 2 * NB]
+        nc.vector.tensor_tensor(out=dd[:, halves[0]], in0=hT_last[:, halves[0]], in1=nn[:, halves[0]], op=ALU.subtract)
+        times_z(LAST - 1, nc.vector)
+        nc.vector.tensor_tensor(out=dd[:, halves[1]], in0=hT_last[:, halves[1]], in1=nn[:, halves[1]], op=ALU.subtract)
+        out_turn(LAST - 1)
+        for cs in halves:
+            nc.vector.tensor_tensor(out=dd[:, cs], in0=gate_of[(LAST, Z)][:, cs], in1=dd[:, cs], op=ALU.mult)
+        copies_out()
+        for a in range(2):
+            po = bank([P, 2, P], F32, "po")
+            for jj in range(2):
+                blk = slice((2 * a + jj) * P, (2 * a + jj + 1) * P)
+                nc.tensor.matmul(po[:, jj, :], lhsT=nn[:, blk], rhs=ident_f[:], is_transpose=True, start=True, stop=False)
+                nc.tensor.matmul(po[:, jj, :], lhsT=dd[:, blk], rhs=ident_f[:], is_transpose=True, start=False, stop=True)
+            osb = stream.tile([P, 2, P], F32, name="osb", tag="osb", bufs=4)
+            if a == 0:
+                nc.scalar.copy(out=osb[:], in_=po[:])
+            else:
+                nc.vector.tensor_copy(out=osb[:], in_=po[:])
+            nc.sync.dma_start(out=outv[:, 4 + 2 * a : 6 + 2 * a, c * P : (c + 1) * P], in_=osb[:])

@@ -52,6 +52,7 @@ def tile_wavernncell_pa_kernel(tc, x, feat, aux1, h, w_ih, w_hh_bytes, w_hh_scal
         ident_f = keep.tile([P, P], F32, name="ident_f")
         ident_b = keep.tile([P, P], BF16, name="ident_b")
         warm = keep.tile([P, 2], F32, name="warm")
+        one = keep.tile([P, 1], F32, name="one")
         hg = keep.tile([P, 2, 4 * B], BF16, name="hg", align_bytes=64)
         hq = keep.tile([P, 2, B], U32, name="hq", align_bytes=64)
         hs = keep.tile([P, 2, B], U8, name="hs", align_bytes=64)
@@ -125,6 +126,7 @@ def tile_wavernncell_pa_kernel(tc, x, feat, aux1, h, w_ih, w_hh_bytes, w_hh_scal
         wbytes_of = {}
         wbf_of = {}
         xw_of = {}
+        sorted_tiles = set()
 
         def w_load(c):
             wbytes = stream.tile([P, 3, H], U8, name="wbytes", tag="wbytes", bufs=4)
@@ -134,7 +136,14 @@ def tile_wavernncell_pa_kernel(tc, x, feat, aux1, h, w_ih, w_hh_bytes, w_hh_scal
         def w_cast(c, q, on_vector=False):
             wbf = stream.tile([P, H], BF16, name="wbf", tag="wbf", bufs=6)
             if on_vector:
-                nc.vector.tensor_copy(out=wbf[:], in_=wbytes_of[c][:, q, :].bitcast(FP8))
+                nc.vector.tensor_scalar(
+                    out=wbf[:].rearrange("p (u w e) -> p w u e", u=2, e=2),
+                    in0=wbytes_of[c][:, q, :].bitcast(FP8).rearrange("p (w u e) -> p w u e", u=2, e=2),
+                    scalar1=one[:],
+                    scalar2=None,
+                    op0=ALU.mult,
+                )
+                sorted_tiles.add((c, q))
             else:
                 nc.scalar.copy(out=wbf[:], in_=wbytes_of[c][:, q, :].bitcast(FP8))
             wbf_of[(c, q)] = wbf
@@ -144,7 +153,11 @@ def tile_wavernncell_pa_kernel(tc, x, feat, aux1, h, w_ih, w_hh_bytes, w_hh_scal
             xt = bank([P, 2, 2, P], F32, "xw")
             for g in range(2):
                 for u in range(2):
-                    nc.tensor.transpose(xt[:, g, u, :], words[:, 256 * g + u : 256 * (g + 1) : 2], ident_f[:])
+                    if (c, q) in sorted_tiles:
+                        run = words[:, 256 * u + P * g : 256 * u + P * (g + 1)]
+                    else:
+                        run = words[:, 256 * g + u : 256 * (g + 1) : 2]
+                    nc.tensor.transpose(xt[:, g, u, :], run, ident_f[:])
             xw_of[(c, q)] = xt
 
         runs = [(0, 2), (2, 1)] + [(3 + 4 * k, 4) for k in range(5)] + [(23, 1)]
@@ -332,6 +345,7 @@ def tile_wavernncell_pa_kernel(tc, x, feat, aux1, h, w_ih, w_hh_bytes, w_hh_scal
             aux_sb = early.tile([P, 8, AUX], BF16, name="aux_sb")
 
             nc.vector.memset(warm[:], 0.0)
+            nc.vector.memset(one[:], 1.0)
             nc.vector.memset(brow[:], 0.0)
             masks.make_identity(nc, ident_f[:])
             masks.make_identity(nc, ident_b[:])

@@ -24,7 +24,10 @@ LAST = UNITS - 1
 R, Z, N = 0, 1, 2
 NAMES = ("r", "z", "n")
 
+
 HELPED = (2, 4, 6, 8, 10, 12, 14)
+VSET = set(range(6, 24))
+VADD = (11, 12, 13, 14, 15)
 
 
 def tile_wavernncell_pa_kernel(tc, x, feat, aux1, h, w_ih, w_hh_bytes, w_hh_scale, b_ih, b_hh, out):
@@ -46,6 +49,7 @@ def tile_wavernncell_pa_kernel(tc, x, feat, aux1, h, w_ih, w_hh_bytes, w_hh_scal
         h_sb = keep.tile([P, 8, H], BF16, name="h_sb")
         wih_sb = [keep.tile([P, SETS, IN], BF16, name="wih_sb%d" % q) for q in range(3)]
         wpad = keep.tile([P, 2, SETS, P], BF16, name="wpad")
+        w1z = keep.tile([P, SETS, 1], F32, name="w1z")
         brow = keep.tile([P, P], BF16, name="brow")
         bcol = keep.tile([P, 48], F32, name="bcol")
         brz = keep.tile([P, 16], F32, name="brz")
@@ -61,7 +65,7 @@ def tile_wavernncell_pa_kernel(tc, x, feat, aux1, h, w_ih, w_hh_bytes, w_hh_scal
         wg3 = [keep.tile([P, 4, H], BF16, name="wg%d" % k, align_bytes=64) for k in range(3)]
         featT = keep.tile([P, B], BF16, name="featT")
         auxT = keep.tile([P, B], BF16, name="auxT")
-        rhs3 = keep.tile([P, B], BF16, name="rhs3")
+        xs = keep.tile([P, B], BF16, name="xs")
         x0f = keep.tile([P, B], F32, name="x0f")
         x1f = keep.tile([P, B], F32, name="x1f")
 
@@ -94,19 +98,6 @@ def tile_wavernncell_pa_kernel(tc, x, feat, aux1, h, w_ih, w_hh_bytes, w_hh_scal
                 in_=hg[:, g, nb * 4 * NB : (nb + 1) * 4 * NB],
             )
 
-        hT_of = {}
-
-        def hT_turn(c):
-            ph = bank([P, 8, P], BF16, "ph")
-            for j in range(8):
-                nc.tensor.transpose(ph[:, j, :], h_sb[:, j, c * P : (c + 1) * P], ident_b[:])
-            pending.append(("hT", c, ph))
-
-        def hT_copy(c, ph):
-            hT = stream.tile([P, B], BF16, name="hT", tag="hT")
-            nc.scalar.copy(out=hT[:], in_=ph[:].rearrange("p j b -> p (j b)"))
-            hT_of[c] = hT
-
         wT_of = {}
 
         def wT_turn(c):
@@ -116,12 +107,14 @@ def tile_wavernncell_pa_kernel(tc, x, feat, aux1, h, w_ih, w_hh_bytes, w_hh_scal
                 nc.tensor.transpose(pw[:, 2 * q + 1, :], wih_sb[q][:, c, FEAT : FEAT + AUX], ident_b[:])
             nc.tensor.transpose(pw[:, 6, :], wpad[:, 0, c, :], ident_b[:])
             nc.tensor.transpose(pw[:, 7, :], wpad[:, 1, c, :], ident_b[:])
-            pending.append(("wT", c, pw))
+            pending.append((c, pw))
 
-        def wT_copy(c, pw):
-            wT = stream.tile([P, 8, P], BF16, name="wT", tag="wT", bufs=4)
-            nc.scalar.copy(out=wT[:], in_=pw[:])
-            wT_of[c] = wT
+        def copies_out():
+            for c, pw in pending:
+                wT = stream.tile([P, 8, P], BF16, name="wT", tag="wT", bufs=4)
+                nc.scalar.copy(out=wT[:], in_=pw[:])
+                wT_of[c] = wT
+            pending.clear()
 
         wbytes_of = {}
         wbf_of = {}
@@ -133,9 +126,9 @@ def tile_wavernncell_pa_kernel(tc, x, feat, aux1, h, w_ih, w_hh_bytes, w_hh_scal
             nc.sync.dma_start(out=wbytes[:], in_=wbv[c, :, :, :])
             wbytes_of[c] = wbytes
 
-        def w_cast(c, q, on_vector=False):
+        def w_cast(c, q):
             wbf = stream.tile([P, H], BF16, name="wbf", tag="wbf", bufs=6)
-            if on_vector:
+            if c < 2 or 3 * c + q in VSET:
                 nc.vector.tensor_scalar(
                     out=wbf[:].rearrange("p (u w e) -> p w u e", u=2, e=2),
                     in0=wbytes_of[c][:, q, :].bitcast(FP8).rearrange("p (w u e) -> p w u e", u=2, e=2),
@@ -189,153 +182,144 @@ def tile_wavernncell_pa_kernel(tc, x, feat, aux1, h, w_ih, w_hh_bytes, w_hh_scal
 
         gi_of = {}
         gh_of = {}
+        sum_of = {}
+        gate_of = {}
 
-        def bank_name(kind, i, q):
-            return kind + NAMES[R if (q == N and i == LAST) else q]
+        def cols_of(i):
+            nb = i % 2
+            return slice(nb * NB, (nb + 1) * NB)
 
-        def mm_gi(i, q, first=True, rest=True):
-            c, nb = i // 2, i % 2
-            cols = slice(nb * NB, (nb + 1) * NB)
+        def mm_gi_r(i):
+            c = i // 2
             wT = wT_of[c]
-            with_x = q == N or (q == R and i in HELPED)
-            if first:
-                nm = bank_name("gi", i, q)
-                ps = acc.tile([P, NB], F32, name=nm, tag=nm)
-                gi_of[(i, q)] = ps
-                nc.tensor.matmul(ps[:], lhsT=wT[:, 2 * q, :], rhs=featT[:, cols], start=True, stop=False)
-            if rest:
-                ps = gi_of[(i, q)]
-                nc.tensor.matmul(ps[:], lhsT=wT[:, 2 * q + 1, :], rhs=auxT[:, cols], start=False, stop=not with_x)
-                if with_x:
-                    nc.tensor.matmul(ps[:], lhsT=wT[:, 6 if q == N else 7, :], rhs=rhs3[:, cols], start=False, stop=True)
+            ps = acc.tile([P, NB], F32, name="gir", tag="gir")
+            gi_of[(i, R)] = ps
+            helped = i in HELPED
+            nc.tensor.matmul(ps[:], lhsT=wT[:, 0, :], rhs=featT[:, cols_of(i)], start=True, stop=False)
+            nc.tensor.matmul(ps[:], lhsT=wT[:, 1, :], rhs=auxT[:, cols_of(i)], start=False, stop=not helped)
+            if helped:
+                nc.tensor.matmul(ps[:], lhsT=wT[:, 7, :], rhs=xs[:, cols_of(i)], start=False, stop=True)
+
+        def mm_gi_t(i, q):
+            c, nb = i // 2, i % 2
+            wT = wT_of[c]
+            nm = "zb" if q == Z else "nb"
+            ps = acc.tile([P, 4, P], F32, name=nm, tag=nm)
+            gi_of[(i, q)] = ps
+            for j in range(4):
+                blk = slice(nb * NB + j * P, nb * NB + (j + 1) * P)
+                nc.tensor.matmul(ps[:, j, :], lhsT=featT[:, blk], rhs=wT[:, 2 * q, :], start=(j == 0), stop=False)
+                nc.tensor.matmul(ps[:, j, :], lhsT=auxT[:, blk], rhs=wT[:, 2 * q + 1, :], start=False, stop=False)
+                if q == N:
+                    nc.tensor.matmul(ps[:, j, :], lhsT=xs[:, blk], rhs=wT[:, 6, :], start=False, stop=False)
+
+        def turn_onto(i, q, tiles):
+            ps = gi_of[(i, q)]
+            for a, t in enumerate(tiles):
+                for j in range(4):
+                    last = a == len(tiles) - 1 and j == 3
+                    nc.tensor.matmul(ps[:, j, :], lhsT=t[:, j * P : (j + 1) * P], rhs=ident_f[:], is_transpose=True, start=False, stop=last)
 
         def mm_gh(i, q):
-            c, nb = i // 2, i % 2
-            cols = slice(nb * NB, (nb + 1) * NB)
-            nm = bank_name("gh", i, q)
+            c = i // 2
+            nm = "gh" + NAMES[q]
             ps = acc.tile([P, NB], F32, name=nm, tag=nm)
             for g in range(2):
                 nc.tensor.matmul_mx(
                     out=ps[:],
                     lhsT=wq[:, 3 * c + q, g * P : (g + 1) * P].bitcast(FP8X4),
                     lhsT_scale=ws[:, 3 * c + q, g * P : (g + 1) * P],
-                    rhs=hq[:, g, cols].bitcast(FP8X4),
-                    rhs_scale=hs[:, g, cols],
+                    rhs=hq[:, g, cols_of(i)].bitcast(FP8X4),
+                    rhs_scale=hs[:, g, cols_of(i)],
                     start=(g == 0),
                     stop=(g == 1),
                 )
             gh_of[(i, q)] = ps
 
-        def mm_rz(i):
-            mm_gi(i, R)
-            mm_gh(i, R)
-            mm_gh(i, Z)
-            mm_gi(i, Z)
-
-        def mm_n(i):
-            mm_gi(i, N, rest=False)
-            mm_gh(i, N)
-            mm_gi(i, N, first=False)
-
-        gate_of = {}
-        sum_of = {}
+        def stt(i, q, xf, col, ps, tag):
+            t = ew.tile([P, NB], F32, name=tag, tag=tag)
+            c = i // 2
+            nc.vector.scalar_tensor_tensor(
+                out=t[:], in0=xf[:, cols_of(i)], scalar=wih_sb[q][:, c, col : col + 1], in1=ps[:], op0=ALU.mult, op1=ALU.add
+            )
+            return t
 
         def r_helped_copy(i):
             c = i // 2
             if i in HELPED:
                 a = ew.tile([P, NB], F32, name="ar", tag="ar")
                 nc.scalar.activation(out=a[:], in_=gi_of[(i, R)][:], func=ACT.Identity, bias=brz[:, c : c + 1], scale=1.0)
-                sum_of[(i, R)] = a
+                sum_of[i] = a
 
-        def rz_empty(i):
-            c, nb = i // 2, i % 2
-            cols = slice(nb * NB, (nb + 1) * NB)
-
-            def gi_half(q):
-                a = ew.tile([P, NB], F32, name="a" + NAMES[q], tag="a" + NAMES[q])
-                nc.vector.scalar_tensor_tensor(
-                    out=a[:], in0=x0f[:, cols], scalar=wih_sb[q][:, c, 256:257], in1=gi_of[(i, q)][:], op0=ALU.mult, op1=ALU.add
-                )
-                sum_of[(i, q)] = a
-
-            def gh_half(q):
-                cc = ew.tile([P, NB], F32, name="c" + NAMES[q], tag="c" + NAMES[q])
-                nc.vector.scalar_tensor_tensor(
-                    out=cc[:], in0=x1f[:, cols], scalar=wih_sb[q][:, c, 257:258], in1=gh_of[(i, q)][:], op0=ALU.mult, op1=ALU.add
-                )
-                sum_of[(i, q, "h")] = cc
-
+        def r_empty(i):
             if i in HELPED:
-                nc.vector.tensor_tensor(out=sum_of[(i, R)][:], in0=sum_of[(i, R)][:], in1=gh_of[(i, R)][:], op=ALU.add)
+                nc.vector.tensor_tensor(out=sum_of[i][:], in0=sum_of[i][:], in1=gh_of[(i, R)][:], op=ALU.add)
             else:
-                gi_half(R)
-                gh_half(R)
-            gh_half(Z)
-            gi_half(Z)
+                sum_of[i] = stt(i, R, x0f, 256, gi_of[(i, R)], "ar")
+                sum_of[(i, "h")] = stt(i, R, x1f, 257, gh_of[(i, R)], "cr")
 
-        def rz_sum(i, q):
-            if not (q == R and i in HELPED):
-                engine = nc.vector if i == LAST else nc.gpsimd
-                engine.tensor_tensor(out=sum_of[(i, q)][:], in0=sum_of[(i, q)][:], in1=sum_of[(i, q, "h")][:], op=ALU.add)
+        def r_sum(i, engine):
+            if i not in HELPED:
+                engine.tensor_tensor(out=sum_of[i][:], in0=sum_of[i][:], in1=sum_of[(i, "h")][:], op=ALU.add)
 
-        def rz_sigmoid(i, q):
+        def r_sigmoid(i):
             c = i // 2
-            gt = ew.tile([P, NB], F32, name="g" + NAMES[q], tag="g" + NAMES[q], bufs=3)
-            if q == R and i in HELPED:
-                nc.scalar.activation(out=gt[:], in_=sum_of[(i, q)][:], func=ACT.Sigmoid)
+            gt = ew.tile([P, NB], F32, name="gr", tag="gr")
+            if i in HELPED:
+                nc.scalar.activation(out=gt[:], in_=sum_of[i][:], func=ACT.Sigmoid)
             else:
-                nc.scalar.activation(out=gt[:], in_=sum_of[(i, q)][:], func=ACT.Sigmoid, bias=brz[:, 8 * q + c : 8 * q + c + 1], scale=1.0)
-            gate_of[(i, q)] = gt
+                nc.scalar.activation(out=gt[:], in_=sum_of[i][:], func=ACT.Sigmoid, bias=brz[:, c : c + 1], scale=1.0)
+            gate_of[(i, R)] = gt
 
-        def n_gate(i):
+        cz_of = {}
+        sz_of = {}
+
+        def z_empty(i):
+            cz_of[i] = stt(i, Z, x0f, 256, gh_of[(i, Z)], "cz")
+
+        def z_side(i):
+            c = i // 2
+            t = ew.tile([P, NB], F32, name="sz", tag="sz")
+            nc.scalar.activation(out=t[:], in_=x1f[:, cols_of(i)], func=ACT.Identity, bias=brz[:, 8 + c : 9 + c], scale=w1z[:, c, :])
+            sz_of[i] = t
+
+        def z_sigmoid(i):
+            gt = ew.tile([P, 4, P], F32, name="gz", tag="gz", bufs=3)
+            nc.scalar.activation(out=gt[:], in_=gi_of[(i, Z)][:], func=ACT.Sigmoid)
+            gate_of[(i, Z)] = gt
+
+        qq_of = {}
+
+        def n_q(i):
             c = i // 2
             qq = ew.tile([P, NB], F32, name="qq", tag="qq")
-            halves = (slice(0, NB // 2), slice(NB // 2, NB))
-            for cs in halves:
-                nc.vector.scalar_tensor_tensor(
-                    out=qq[:, cs], in0=gh_of[(i, N)][:, cs], scalar=bcol[:, 40 + c : 41 + c], in1=gate_of[(i, R)][:, cs], op0=ALU.add, op1=ALU.mult
-                )
-            for cs in halves:
-                nc.vector.tensor_tensor(out=qq[:, cs], in0=qq[:, cs], in1=gi_of[(i, N)][:, cs], op=ALU.add)
-            nn = ew.tile([P, NB], F32, name="nn", tag="nn", bufs=4)
-            nc.scalar.activation(out=nn[:], in_=qq[:], func=ACT.Tanh, bias=bcol[:, 16 + c : 17 + c], scale=1.0)
+            nc.vector.scalar_tensor_tensor(
+                out=qq[:], in0=gh_of[(i, N)][:], scalar=bcol[:, 40 + c : 41 + c], in1=gate_of[(i, R)][:], op0=ALU.add, op1=ALU.mult
+            )
+            qq_of[i] = qq
+
+        def n_tanh(i):
+            nn = ew.tile([P, 4, P], F32, name="nn", tag="nn", bufs=3)
+            nc.scalar.activation(out=nn[:], in_=gi_of[(i, N)][:], func=ACT.Tanh)
             gate_of[(i, N)] = nn
 
         dd_of = {}
 
         def h_minus_n(i, engine):
             c, nb = i // 2, i % 2
-            cols = slice(nb * NB, (nb + 1) * NB)
-            dd = ew.tile([P, NB], F32, name="dd", tag="dd", bufs=3)
-            engine.tensor_tensor(out=dd[:], in0=hT_of[c][:, cols], in1=gate_of[(i, N)][:], op=ALU.subtract)
+            dd = stream.tile([P, 4, P], F32, name="dd", tag="dd", bufs=4)
+            engine.tensor_tensor(out=dd[:], in0=h_sb[:, 4 * nb : 4 * nb + 4, c * P : (c + 1) * P], in1=gate_of[(i, N)][:], op=ALU.subtract)
             dd_of[i] = dd
 
         def times_z(i, engine):
             engine.tensor_tensor(out=dd_of[i][:], in0=gate_of[(i, Z)][:], in1=dd_of[i][:], op=ALU.mult)
 
-        def out_turn(i):
-            po = bank([P, 4, P], F32, "po")
-            for jj in range(4):
-                blk = slice(jj * P, (jj + 1) * P)
-                nc.tensor.matmul(po[:, jj, :], lhsT=gate_of[(i, N)][:, blk], rhs=ident_f[:], is_transpose=True, start=True, stop=False)
-                nc.tensor.matmul(po[:, jj, :], lhsT=dd_of[i][:, blk], rhs=ident_f[:], is_transpose=True, start=False, stop=True)
-            pending.append(("out", i, po))
+        def plus_n(i, engine):
+            engine.tensor_tensor(out=dd_of[i][:], in0=gate_of[(i, N)][:], in1=dd_of[i][:], op=ALU.add)
 
-        def out_store(i, po):
+        def store(i):
             c, nb = i // 2, i % 2
-            osb = stream.tile([P, 4, P], F32, name="osb", tag="osb", bufs=4)
-            nc.scalar.copy(out=osb[:], in_=po[:])
-            nc.sync.dma_start(out=outv[:, 4 * nb : 4 * nb + 4, c * P : (c + 1) * P], in_=osb[:])
-
-        def copies_out():
-            for what, index, ps in pending:
-                if what == "hT":
-                    hT_copy(index, ps)
-                elif what == "wT":
-                    wT_copy(index, ps)
-                else:
-                    out_store(index, ps)
-            pending.clear()
+            nc.sync.dma_start(out=outv[:, 4 * nb : 4 * nb + 4, c * P : (c + 1) * P], in_=dd_of[i][:])
 
         ctx.enter_context(tc.manual_schedule())
 
@@ -350,6 +334,7 @@ def tile_wavernncell_pa_kernel(tc, x, feat, aux1, h, w_ih, w_hh_bytes, w_hh_scal
             masks.make_identity(nc, ident_f[:])
             masks.make_identity(nc, ident_b[:])
             nc.gpsimd.memset(wpad[:], 0.0)
+            nc.gpsimd.memset(xs[64:128, :], 1.0)
 
             w_load(0)
             nc.scalar.dma_start(out=s4[:].rearrange("p g o t -> p (g o) t"), in_=w_hh_scale.rearrange("o (g p t) -> p (o g) t", g=2, p=P, t=4))
@@ -357,13 +342,13 @@ def tile_wavernncell_pa_kernel(tc, x, feat, aux1, h, w_ih, w_hh_bytes, w_hh_scal
             nc.sync.dma_start(out=h_sb[:, 0:2, :], in_=hv[:, 0:2, :])
             nc.sync.dma_start(out=h_sb[:, 2:4, :], in_=hv[:, 2:4, :])
             w_load(1)
+            nc.sync.dma_start(out=brow[0:24, :], in_=b_ih.rearrange("(r m) -> r m", m=P))
+            nc.sync.dma_start(out=brow[24:48, :], in_=b_hh.rearrange("(r m) -> r m", m=P))
             nc.sync.dma_start(out=feat_sb[:].rearrange("p j f -> p (j f)"), in_=feat.rearrange("(p j) f -> p (j f)", j=8))
             nc.sync.dma_start(out=aux_sb[:].rearrange("p j f -> p (j f)"), in_=aux1.rearrange("(p j) f -> p (j f)", j=8))
             for q in range(3):
                 nc.sync.dma_start(out=wih_sb[q][:, 0:4, :], in_=wihv[q, :, 0:4, :])
             nc.sync.dma_start(out=xb[:], in_=x.rearrange("b e -> (b e)").partition_broadcast(P))
-            nc.sync.dma_start(out=brow[0:24, :], in_=b_ih.rearrange("(r m) -> r m", m=P))
-            nc.sync.dma_start(out=brow[24:48, :], in_=b_hh.rearrange("(r m) -> r m", m=P))
             nc.sync.dma_start(out=h_sb[:, 4:6, :], in_=hv[:, 4:6, :])
             nc.sync.dma_start(out=h_sb[:, 6:8, :], in_=hv[:, 6:8, :])
             w_load(2)
@@ -378,14 +363,17 @@ def tile_wavernncell_pa_kernel(tc, x, feat, aux1, h, w_ih, w_hh_bytes, w_hh_scal
                     nc.gpsimd.tensor_scalar(
                         out=xf[:].rearrange("q (j p) -> q j p", j=8), in0=xv[:, e, :, :], scalar1=1.0, scalar2=0.0, op0=ALU.mult, op1=ALU.add
                     )
-                nc.gpsimd.tensor_scalar(out=rhs3[:], in0=x0f[:], scalar1=1.0, scalar2=0.0, op0=ALU.mult, op1=ALU.add)
-                nc.gpsimd.tensor_scalar(out=rhs3[32:64, :], in0=x1f[32:64, :], scalar1=1.0, scalar2=0.0, op0=ALU.mult, op1=ALU.add)
+                nc.gpsimd.tensor_scalar(out=xs[0:32, :], in0=x0f[0:32, :], scalar1=1.0, scalar2=0.0, op0=ALU.mult, op1=ALU.add)
+                nc.gpsimd.tensor_scalar(out=xs[32:64, :], in0=x1f[32:64, :], scalar1=1.0, scalar2=0.0, op0=ALU.mult, op1=ALU.add)
 
             def wpad_fill(half):
                 cs = slice(4 * half, 4 * half + 4)
                 for a, q in enumerate((N, R)):
                     nc.gpsimd.tensor_copy(out=wpad[:, a, cs, 0:1], in_=wih_sb[q][:, cs, 256:257])
                     nc.gpsimd.tensor_copy(out=wpad[:, a, cs, 32:33], in_=wih_sb[q][:, cs, 257:258])
+                nc.gpsimd.tensor_copy(out=w1z[:, cs, :], in_=wih_sb[Z][:, cs, 257:258])
+                if half == 0:
+                    nc.gpsimd.tensor_copy(out=wpad[:, 0, :, 64:65], in_=bcol[:, 16:24].rearrange("p (c o) -> p c o", o=1))
 
             def feat_aux_turn(half):
                 for src, dst in ((feat_sb, featT), (aux_sb, auxT)):
@@ -397,12 +385,12 @@ def tile_wavernncell_pa_kernel(tc, x, feat, aux1, h, w_ih, w_hh_bytes, w_hh_scal
             def bias_turn():
                 pb = bank([P, P], BF16, "pb")
                 nc.tensor.transpose(pb[:], brow[:], ident_b[:])
-                nc.vector.tensor_copy(out=bcol[:], in_=pb[:, 0:48])
-                nc.vector.tensor_tensor(out=brz[:], in0=bcol[:, 0:16], in1=bcol[:, 24:40], op=ALU.add)
+                nc.scalar.copy(out=bcol[:], in_=pb[:, 0:48])
+                nc.gpsimd.tensor_tensor(out=brz[:], in0=bcol[:, 0:16], in1=bcol[:, 24:40], op=ALU.add)
 
-            spare_banks.extend(["tr", "tr", "ghn", "gin", "ghz", "ghr"])
+            spare_banks.extend(["tr", "tr", "ghn", "nb", "ghz", "ghr"])
             for q in range(3):
-                w_cast(0, q, on_vector=True)
+                w_cast(0, q)
             for q in range(3):
                 w_turn(0, q)
             for jp in range(2):
@@ -411,7 +399,8 @@ def tile_wavernncell_pa_kernel(tc, x, feat, aux1, h, w_ih, w_hh_bytes, w_hh_scal
             for q in range(3):
                 w_scale(0, q)
             for q in range(3):
-                w_cast(1, q, on_vector=True)
+                w_cast(1, q)
+            bias_turn()
             for q in range(3):
                 w_turn(1, q)
             feat_aux_turn(0)
@@ -427,7 +416,6 @@ def tile_wavernncell_pa_kernel(tc, x, feat, aux1, h, w_ih, w_hh_bytes, w_hh_scal
             h_quantize(1, 0)
             for q in range(3):
                 w_scale(1, q)
-            bias_turn()
             spare_banks.clear()
 
             cast_in = {}
@@ -438,45 +426,55 @@ def tile_wavernncell_pa_kernel(tc, x, feat, aux1, h, w_ih, w_hh_bytes, w_hh_scal
             def is_unit(i):
                 return 0 <= i < UNITS
 
-            def step(tau, after_rz_empty=None, with_out=True):
+            def step(tau, after_empty=None):
                 copies_out()
                 if is_unit(tau):
-                    rz_sigmoid(tau, Z)
+                    z_sigmoid(tau)
                 for c, q in cast_in.get(tau, ()):
                     if q == R and c + 2 < SETS:
                         w_load(c + 2)
-                    w_cast(c, q)
                 if is_unit(tau - 1):
                     h_minus_n(tau - 1, nc.gpsimd)
+                if is_unit(tau + 1):
+                    r_empty(tau + 1)
+                    z_empty(tau + 1)
+                if is_unit(tau):
+                    n_q(tau)
+                if is_unit(tau + 1):
+                    r_sum(tau + 1, nc.gpsimd)
                 for c, q in cast_in.get(tau - 2, ()):
                     w_scale(c, q)
-                if is_unit(tau + 1):
-                    rz_empty(tau + 1)
-                if after_rz_empty is not None:
-                    after_rz_empty()
+                if after_empty is not None:
+                    after_empty()
                 if is_unit(tau + 2):
-                    mm_rz(tau + 2)
+                    mm_gi_r(tau + 2)
                     r_helped_copy(tau + 2)
+                    mm_gh(tau + 2, R)
+                    mm_gh(tau + 2, Z)
+                if is_unit(tau + 1):
+                    mm_gh(tau + 1, N)
+                if is_unit(tau):
+                    mm_gi_t(tau, N)
+                    turn_onto(tau, N, [qq_of[tau]])
+                    n_tanh(tau)
                 for c, q in cast_in.get(tau - 1, ()):
                     w_turn(c, q)
-                if is_unit(tau):
-                    n_gate(tau)
                 if is_unit(tau + 1):
-                    mm_n(tau + 1)
-                    rz_sum(tau + 1, R)
-                    rz_sigmoid(tau + 1, R)
+                    mm_gi_t(tau + 1, Z)
+                    turn_onto(tau + 1, Z, [sz_of[tau + 1], cz_of[tau + 1]])
+                    r_sigmoid(tau + 1)
+                if is_unit(tau + 2):
+                    z_side(tau + 2)
+                for c, q in cast_in.get(tau, ()):
+                    w_cast(c, q)
                 if is_unit(tau - 1):
                     times_z(tau - 1, nc.gpsimd)
-                if is_unit(tau + 1):
-                    rz_sum(tau + 1, Z)
+                    plus_n(tau - 1, nc.vector if tau - 1 in VADD else nc.gpsimd)
+                    store(tau - 1)
                 for c, q in cast_in.get(tau - 2, ()):
                     w_quantize(c, q)
                 if tau % 2 == 1 and 2 <= (tau + 5) // 2 < SETS:
                     wT_turn((tau + 5) // 2)
-                if tau % 2 == 0 and 1 <= (tau + 2) // 2 < SETS:
-                    hT_turn((tau + 2) // 2)
-                if is_unit(tau - 1) and with_out:
-                    out_turn(tau - 1)
 
             def quantize_second_half():
                 h_quantize(0, 1)
@@ -484,7 +482,7 @@ def tile_wavernncell_pa_kernel(tc, x, feat, aux1, h, w_ih, w_hh_bytes, w_hh_scal
 
             step(-3)
             step(-2)
-            spare_banks.extend(["ghn", "gin"])
+            spare_banks.extend(["ghn", "nb", "zb"])
             for jp in range(2, 4):
                 for g in range(2):
                     h_turn(jp, g)
@@ -493,60 +491,7 @@ def tile_wavernncell_pa_kernel(tc, x, feat, aux1, h, w_ih, w_hh_bytes, w_hh_scal
             for q in range(3):
                 w_quantize(1, q)
             step(-1, quantize_second_half)
-            hT_turn(0)
             wpad_fill(1)
 
-        for tau in range(0, LAST - 2):
+        for tau in range(0, LAST + 2):
             step(tau)
-        step(LAST - 2, with_out=False)
-
-        copies_out()
-        h_minus_n(LAST - 2, nc.gpsimd)
-        rz_empty(LAST)
-        rz_sum(LAST, R)
-        rz_sum(LAST, Z)
-        mm_n(LAST)
-        out_turn(LAST - 3)
-        rz_sigmoid(LAST, R)
-        rz_sigmoid(LAST - 1, Z)
-        rz_sigmoid(LAST, Z)
-        n_gate(LAST - 1)
-        copies_out()
-        times_z(LAST - 2, nc.gpsimd)
-        c = LAST // 2
-        qq = ew.tile([P, NB], F32, name="qq", tag="qq")
-        nn = ew.tile([P, NB], F32, name="nn", tag="nn", bufs=4)
-        dd = ew.tile([P, NB], F32, name="dd", tag="dd", bufs=3)
-        halves = (slice(0, NB // 2), slice(NB // 2, NB))
-        for cs in halves:
-            nc.vector.scalar_tensor_tensor(
-                out=qq[:, cs], in0=gh_of[(LAST, N)][:, cs], scalar=bcol[:, 40 + c : 41 + c], in1=gate_of[(LAST, R)][:, cs], op0=ALU.add, op1=ALU.mult
-            )
-        for cs in halves:
-            nc.vector.tensor_tensor(out=qq[:, cs], in0=qq[:, cs], in1=gi_of[(LAST, N)][:, cs], op=ALU.add)
-            nc.scalar.activation(out=nn[:, cs], in_=qq[:, cs], func=ACT.Tanh, bias=bcol[:, 16 + c : 17 + c], scale=1.0)
-        spare_used[0] = 0
-        spare_banks.extend(["tr", "giz", "ghz", "gin"])
-        out_turn(LAST - 2)
-        h_minus_n(LAST - 1, nc.vector)
-        copies_out()
-        hT_last = hT_of[c][:, NB : 2 * NB]
-        nc.vector.tensor_tensor(out=dd[:, halves[0]], in0=hT_last[:, halves[0]], in1=nn[:, halves[0]], op=ALU.subtract)
-        times_z(LAST - 1, nc.vector)
-        nc.vector.tensor_tensor(out=dd[:, halves[1]], in0=hT_last[:, halves[1]], in1=nn[:, halves[1]], op=ALU.subtract)
-        out_turn(LAST - 1)
-        for cs in halves:
-            nc.vector.tensor_tensor(out=dd[:, cs], in0=gate_of[(LAST, Z)][:, cs], in1=dd[:, cs], op=ALU.mult)
-        copies_out()
-        for a in range(2):
-            po = bank([P, 2, P], F32, "po")
-            for jj in range(2):
-                blk = slice((2 * a + jj) * P, (2 * a + jj + 1) * P)
-                nc.tensor.matmul(po[:, jj, :], lhsT=nn[:, blk], rhs=ident_f[:], is_transpose=True, start=True, stop=False)
-                nc.tensor.matmul(po[:, jj, :], lhsT=dd[:, blk], rhs=ident_f[:], is_transpose=True, start=False, stop=True)
-            osb = stream.tile([P, 2, P], F32, name="osb", tag="osb", bufs=4)
-            if a == 0:
-                nc.scalar.copy(out=osb[:], in_=po[:])
-            else:
-                nc.vector.tensor_copy(out=osb[:], in_=po[:])
-            nc.sync.dma_start(out=outv[:, 4 + 2 * a : 6 + 2 * a, c * P : (c + 1) * P], in_=osb[:])

@@ -21,13 +21,14 @@ NB = 512
 SETS = 8
 UNITS = 2 * SETS
 LAST = UNITS - 1
+ROW = 272
 R, Z, N = 0, 1, 2
 NAMES = ("r", "z", "n")
 
 
-HELPED = (2, 4, 6, 8, 10, 12, 14)
-VSET = set(range(6, 24))
-VADD = (11, 12, 13, 14, 15)
+RH = ()
+ZH = (3, 5, 7, 9, 11, 13, 15)
+VADD = tuple(range(7, 15))
 
 
 def tile_wavernncell_pa_kernel(tc, x, feat, aux1, h, w_ih, w_hh_bytes, w_hh_scale, b_ih, b_hh, out):
@@ -47,7 +48,7 @@ def tile_wavernncell_pa_kernel(tc, x, feat, aux1, h, w_ih, w_hh_bytes, w_hh_scal
 
         s4 = keep.tile([P, 2, 1, 4], F32, name="s4")
         h_sb = keep.tile([P, 8, H], BF16, name="h_sb")
-        wih_sb = [keep.tile([P, SETS, IN], BF16, name="wih_sb%d" % q) for q in range(3)]
+        wih_sb = [keep.tile([P, SETS, ROW], BF16, name="wih_sb%d" % q) for q in range(3)]
         wpad = keep.tile([P, 2, SETS, P], BF16, name="wpad")
         w1z = keep.tile([P, SETS, 1], F32, name="w1z")
         brow = keep.tile([P, P], BF16, name="brow")
@@ -66,8 +67,8 @@ def tile_wavernncell_pa_kernel(tc, x, feat, aux1, h, w_ih, w_hh_bytes, w_hh_scal
         featT = keep.tile([P, B], BF16, name="featT")
         auxT = keep.tile([P, B], BF16, name="auxT")
         xs = keep.tile([P, B], BF16, name="xs")
-        x0f = keep.tile([P, B], F32, name="x0f")
-        x1f = keep.tile([P, B], F32, name="x1f")
+        x0f = keep.tile([P, B], BF16, name="x0f")
+        x1f = keep.tile([P, B], BF16, name="x1f")
 
         spare_banks = []
         spare_used = [0]
@@ -128,7 +129,7 @@ def tile_wavernncell_pa_kernel(tc, x, feat, aux1, h, w_ih, w_hh_bytes, w_hh_scal
 
         def w_cast(c, q):
             wbf = stream.tile([P, H], BF16, name="wbf", tag="wbf", bufs=6)
-            if c < 2 or 3 * c + q in VSET:
+            if 3 * c + q < 7:
                 nc.vector.tensor_scalar(
                     out=wbf[:].rearrange("p (u w e) -> p w u e", u=2, e=2),
                     in0=wbytes_of[c][:, q, :].bitcast(FP8).rearrange("p (w u e) -> p w u e", u=2, e=2),
@@ -153,7 +154,7 @@ def tile_wavernncell_pa_kernel(tc, x, feat, aux1, h, w_ih, w_hh_bytes, w_hh_scal
                     nc.tensor.transpose(xt[:, g, u, :], run, ident_f[:])
             xw_of[(c, q)] = xt
 
-        runs = [(0, 2), (2, 1)] + [(3 + 4 * k, 4) for k in range(5)] + [(23, 1)]
+        runs = [(0, 2), (2, 1), (3, 2), (5, 2), (7, 2), (9, 2), (11, 4), (15, 4), (19, 4), (23, 1)]
         run_of = {}
         for k, (first_tile, width) in enumerate(runs):
             for a in range(width):
@@ -194,35 +195,38 @@ def tile_wavernncell_pa_kernel(tc, x, feat, aux1, h, w_ih, w_hh_bytes, w_hh_scal
             wT = wT_of[c]
             ps = acc.tile([P, NB], F32, name="gir", tag="gir")
             gi_of[(i, R)] = ps
-            helped = i in HELPED
+            helped = i in RH
             nc.tensor.matmul(ps[:], lhsT=wT[:, 0, :], rhs=featT[:, cols_of(i)], start=True, stop=False)
             nc.tensor.matmul(ps[:], lhsT=wT[:, 1, :], rhs=auxT[:, cols_of(i)], start=False, stop=not helped)
             if helped:
                 nc.tensor.matmul(ps[:], lhsT=wT[:, 7, :], rhs=xs[:, cols_of(i)], start=False, stop=True)
 
-        def mm_gi_t(i, q):
+        def mm_gi_t(i, q, half=None):
             c, nb = i // 2, i % 2
             wT = wT_of[c]
-            nm = "zb" if q == Z else "nb"
-            ps = acc.tile([P, 4, P], F32, name=nm, tag=nm)
-            gi_of[(i, q)] = ps
-            for j in range(4):
+            nm = "zb" if q == Z else ("gir" if half == 1 else "nb")
+            ps = acc.tile([P, 4, P], F32, name=nm + "t", tag=nm)
+            gi_of[(i, q, half)] = ps
+            first = 2 if half == 1 else 0
+            for j in range(first, 2 if half == 0 else 4):
                 blk = slice(nb * NB + j * P, nb * NB + (j + 1) * P)
-                nc.tensor.matmul(ps[:, j, :], lhsT=featT[:, blk], rhs=wT[:, 2 * q, :], start=(j == 0), stop=False)
+                nc.tensor.matmul(ps[:, j, :], lhsT=featT[:, blk], rhs=wT[:, 2 * q, :], start=(j == first), stop=False)
                 nc.tensor.matmul(ps[:, j, :], lhsT=auxT[:, blk], rhs=wT[:, 2 * q + 1, :], start=False, stop=False)
-                if q == N:
-                    nc.tensor.matmul(ps[:, j, :], lhsT=xs[:, blk], rhs=wT[:, 6, :], start=False, stop=False)
+                if q == N or i in ZH:
+                    nc.tensor.matmul(ps[:, j, :], lhsT=xs[:, blk], rhs=wT[:, 7 if q == N else 6, :], start=False, stop=False)
 
-        def turn_onto(i, q, tiles):
-            ps = gi_of[(i, q)]
+        def turn_onto(i, q, tiles, half=None):
+            ps = gi_of[(i, q, half)]
+            js = range(2 if half == 1 else 0, 2 if half == 0 else 4)
+            tiles = [t for t in tiles if t is not None]
             for a, t in enumerate(tiles):
-                for j in range(4):
-                    last = a == len(tiles) - 1 and j == 3
+                for j in js:
+                    last = a == len(tiles) - 1 and j == js[-1]
                     nc.tensor.matmul(ps[:, j, :], lhsT=t[:, j * P : (j + 1) * P], rhs=ident_f[:], is_transpose=True, start=False, stop=last)
 
         def mm_gh(i, q):
             c = i // 2
-            nm = "gh" + NAMES[q]
+            nm = "gh" + NAMES[R if q == N and i == LAST else q]
             ps = acc.tile([P, NB], F32, name=nm, tag=nm)
             for g in range(2):
                 nc.tensor.matmul_mx(
@@ -246,26 +250,26 @@ def tile_wavernncell_pa_kernel(tc, x, feat, aux1, h, w_ih, w_hh_bytes, w_hh_scal
 
         def r_helped_copy(i):
             c = i // 2
-            if i in HELPED:
+            if i in RH:
                 a = ew.tile([P, NB], F32, name="ar", tag="ar")
                 nc.scalar.activation(out=a[:], in_=gi_of[(i, R)][:], func=ACT.Identity, bias=brz[:, c : c + 1], scale=1.0)
                 sum_of[i] = a
 
         def r_empty(i):
-            if i in HELPED:
+            if i in RH:
                 nc.vector.tensor_tensor(out=sum_of[i][:], in0=sum_of[i][:], in1=gh_of[(i, R)][:], op=ALU.add)
             else:
                 sum_of[i] = stt(i, R, x0f, 256, gi_of[(i, R)], "ar")
                 sum_of[(i, "h")] = stt(i, R, x1f, 257, gh_of[(i, R)], "cr")
 
         def r_sum(i, engine):
-            if i not in HELPED:
+            if i not in RH:
                 engine.tensor_tensor(out=sum_of[i][:], in0=sum_of[i][:], in1=sum_of[(i, "h")][:], op=ALU.add)
 
         def r_sigmoid(i):
             c = i // 2
             gt = ew.tile([P, NB], F32, name="gr", tag="gr")
-            if i in HELPED:
+            if i in RH:
                 nc.scalar.activation(out=gt[:], in_=sum_of[i][:], func=ACT.Sigmoid)
             else:
                 nc.scalar.activation(out=gt[:], in_=sum_of[i][:], func=ACT.Sigmoid, bias=brz[:, c : c + 1], scale=1.0)
@@ -275,17 +279,24 @@ def tile_wavernncell_pa_kernel(tc, x, feat, aux1, h, w_ih, w_hh_bytes, w_hh_scal
         sz_of = {}
 
         def z_empty(i):
-            cz_of[i] = stt(i, Z, x0f, 256, gh_of[(i, Z)], "cz")
+            if i not in ZH:
+                cz_of[i] = stt(i, Z, x0f, 256, gh_of[(i, Z)], "cz")
 
         def z_side(i):
             c = i // 2
+            if i in ZH:
+                sz_of[i] = None
+                t = ew.tile([P, NB], F32, name="cz", tag="cz")
+                nc.scalar.copy(out=t[:], in_=gh_of[(i, Z)][:])
+                cz_of[i] = t
+                return
             t = ew.tile([P, NB], F32, name="sz", tag="sz")
             nc.scalar.activation(out=t[:], in_=x1f[:, cols_of(i)], func=ACT.Identity, bias=brz[:, 8 + c : 9 + c], scale=w1z[:, c, :])
             sz_of[i] = t
 
         def z_sigmoid(i):
-            gt = ew.tile([P, 4, P], F32, name="gz", tag="gz", bufs=3)
-            nc.scalar.activation(out=gt[:], in_=gi_of[(i, Z)][:], func=ACT.Sigmoid)
+            gt = ew.tile([P, 4, P], F32, name="gz", tag="gz", bufs=4)
+            nc.scalar.activation(out=gt[:], in_=gi_of[(i, Z, None)][:], func=ACT.Sigmoid)
             gate_of[(i, Z)] = gt
 
         qq_of = {}
@@ -299,15 +310,15 @@ def tile_wavernncell_pa_kernel(tc, x, feat, aux1, h, w_ih, w_hh_bytes, w_hh_scal
             qq_of[i] = qq
 
         def n_tanh(i):
-            nn = ew.tile([P, 4, P], F32, name="nn", tag="nn", bufs=3)
-            nc.scalar.activation(out=nn[:], in_=gi_of[(i, N)][:], func=ACT.Tanh)
+            nn = ew.tile([P, 4, P], F32, name="nn", tag="nn", bufs=4)
+            nc.scalar.activation(out=nn[:], in_=gi_of[(i, N, None)][:], func=ACT.Tanh)
             gate_of[(i, N)] = nn
 
         dd_of = {}
 
         def h_minus_n(i, engine):
             c, nb = i // 2, i % 2
-            dd = stream.tile([P, 4, P], F32, name="dd", tag="dd", bufs=4)
+            dd = stream.tile([P, 4, P], F32, name="dd", tag="dd", bufs=5)
             engine.tensor_tensor(out=dd[:], in0=h_sb[:, 4 * nb : 4 * nb + 4, c * P : (c + 1) * P], in1=gate_of[(i, N)][:], op=ALU.subtract)
             dd_of[i] = dd
 
@@ -324,7 +335,7 @@ def tile_wavernncell_pa_kernel(tc, x, feat, aux1, h, w_ih, w_hh_bytes, w_hh_scal
         ctx.enter_context(tc.manual_schedule())
 
         with tc.tile_pool(name="early", bufs=1) as early:
-            xb = early.tile([P, 2 * B], BF16, name="xb")
+            x_sb = early.tile([P, 8, NS], BF16, name="x_sb")
             feat_sb = early.tile([P, 8, FEAT], BF16, name="feat_sb")
             aux_sb = early.tile([P, 8, AUX], BF16, name="aux_sb")
 
@@ -333,47 +344,44 @@ def tile_wavernncell_pa_kernel(tc, x, feat, aux1, h, w_ih, w_hh_bytes, w_hh_scal
             nc.vector.memset(brow[:], 0.0)
             masks.make_identity(nc, ident_f[:])
             masks.make_identity(nc, ident_b[:])
-            nc.gpsimd.memset(wpad[:], 0.0)
-            nc.gpsimd.memset(xs[64:128, :], 1.0)
+            nc.vector.memset(wpad[:].rearrange("p a c m -> p (a c m)").bitcast(F32), 0.0)
+            nc.vector.memset(xs[64:128, :], 1.0)
 
             w_load(0)
             nc.scalar.dma_start(out=s4[:].rearrange("p g o t -> p (g o) t"), in_=w_hh_scale.rearrange("o (g p t) -> p (o g) t", g=2, p=P, t=4))
             nc.scalar.activation(out=warm[:, 1:2], in_=warm[:, 0:1], func=ACT.Sigmoid)
             nc.sync.dma_start(out=h_sb[:, 0:2, :], in_=hv[:, 0:2, :])
             nc.sync.dma_start(out=h_sb[:, 2:4, :], in_=hv[:, 2:4, :])
-            w_load(1)
-            nc.sync.dma_start(out=brow[0:24, :], in_=b_ih.rearrange("(r m) -> r m", m=P))
-            nc.sync.dma_start(out=brow[24:48, :], in_=b_hh.rearrange("(r m) -> r m", m=P))
+            nc.scalar.dma_start(out=x_sb[:], in_=x.rearrange("(p j) e -> p j e", j=8))
+            for k, b in enumerate((b_ih, b_hh)):
+                rows = b.rearrange("(r m) -> r m", m=P)
+                nc.scalar.dma_start(out=brow[24 * k : 24 * k + 16, :], in_=rows[0:16, :])
+                nc.scalar.dma_start(out=brow[24 * k + 16 : 24 * k + 24, :], in_=rows[16:24, :])
             nc.sync.dma_start(out=feat_sb[:].rearrange("p j f -> p (j f)"), in_=feat.rearrange("(p j) f -> p (j f)", j=8))
             nc.sync.dma_start(out=aux_sb[:].rearrange("p j f -> p (j f)"), in_=aux1.rearrange("(p j) f -> p (j f)", j=8))
             for q in range(3):
-                nc.sync.dma_start(out=wih_sb[q][:, 0:4, :], in_=wihv[q, :, 0:4, :])
-            nc.sync.dma_start(out=xb[:], in_=x.rearrange("b e -> (b e)").partition_broadcast(P))
+                nc.sync.dma_start(out=wih_sb[q][:, 0:2, 0:IN], in_=wihv[q, :, 0:2, :])
+            w_load(1)
             nc.sync.dma_start(out=h_sb[:, 4:6, :], in_=hv[:, 4:6, :])
             nc.sync.dma_start(out=h_sb[:, 6:8, :], in_=hv[:, 6:8, :])
             w_load(2)
-            w_load(3)
             for q in range(3):
-                nc.sync.dma_start(out=wih_sb[q][:, 4:8, :], in_=wihv[q, :, 4:8, :])
+                nc.sync.dma_start(out=wih_sb[q][:, 2:8, 0:IN], in_=wihv[q, :, 2:8, :])
+            w_load(3)
 
-            xv = xb[:].rearrange("q (p j e) -> q e j p", j=8, e=2)
-
-            def x_spread():
+            def x_turn():
                 for e, xf in enumerate((x0f, x1f)):
-                    nc.gpsimd.tensor_scalar(
-                        out=xf[:].rearrange("q (j p) -> q j p", j=8), in0=xv[:, e, :, :], scalar1=1.0, scalar2=0.0, op0=ALU.mult, op1=ALU.add
-                    )
-                nc.gpsimd.tensor_scalar(out=xs[0:32, :], in0=x0f[0:32, :], scalar1=1.0, scalar2=0.0, op0=ALU.mult, op1=ALU.add)
-                nc.gpsimd.tensor_scalar(out=xs[32:64, :], in0=x1f[32:64, :], scalar1=1.0, scalar2=0.0, op0=ALU.mult, op1=ALU.add)
+                    px = bank([P, 8, P], BF16, "px")
+                    for j in range(8):
+                        nc.tensor.transpose(px[:, j, :], x_sb[:, j, e : e + 1].to_broadcast([P, P]), ident_b[:])
+                    spread = px[:].rearrange("p j b -> p (j b)")
+                    nc.scalar.copy(out=xf[:], in_=spread)
+                    nc.scalar.copy(out=xs[32 * e : 32 * e + 32, :], in_=spread[32 * e : 32 * e + 32, :])
 
-            def wpad_fill(half):
-                cs = slice(4 * half, 4 * half + 4)
-                for a, q in enumerate((N, R)):
-                    nc.gpsimd.tensor_copy(out=wpad[:, a, cs, 0:1], in_=wih_sb[q][:, cs, 256:257])
-                    nc.gpsimd.tensor_copy(out=wpad[:, a, cs, 32:33], in_=wih_sb[q][:, cs, 257:258])
-                nc.gpsimd.tensor_copy(out=w1z[:, cs, :], in_=wih_sb[Z][:, cs, 257:258])
-                if half == 0:
-                    nc.gpsimd.tensor_copy(out=wpad[:, 0, :, 64:65], in_=bcol[:, 16:24].rearrange("p (c o) -> p c o", o=1))
+            def wpad_fill(cs):
+                for a, q in enumerate((Z, N)):
+                    nc.scalar.copy(out=wpad[:, a, cs, 0:33:32], in_=wih_sb[q][:, cs, 256:258])
+                nc.scalar.copy(out=w1z[:, cs, :], in_=wih_sb[Z][:, cs, 257:258])
 
             def feat_aux_turn(half):
                 for src, dst in ((feat_sb, featT), (aux_sb, auxT)):
@@ -388,7 +396,7 @@ def tile_wavernncell_pa_kernel(tc, x, feat, aux1, h, w_ih, w_hh_bytes, w_hh_scal
                 nc.scalar.copy(out=bcol[:], in_=pb[:, 0:48])
                 nc.gpsimd.tensor_tensor(out=brz[:], in0=bcol[:, 0:16], in1=bcol[:, 24:40], op=ALU.add)
 
-            spare_banks.extend(["tr", "tr", "ghn", "nb", "ghz", "ghr"])
+            spare_banks.extend(["tr", "tr", "ghn", "nb", "zb", "ghz", "ghr", "gir"])
             for q in range(3):
                 w_cast(0, q)
             for q in range(3):
@@ -396,102 +404,144 @@ def tile_wavernncell_pa_kernel(tc, x, feat, aux1, h, w_ih, w_hh_bytes, w_hh_scal
             for jp in range(2):
                 for g in range(2):
                     h_turn(jp, g)
+            bias_turn()
+            nc.scalar.copy(out=wpad[:, :, :, 64], in_=bcol[:, 8:24].rearrange("p (a c) -> p a c", a=2))
+            nc.scalar.copy(out=wpad[:, 0, :, 96], in_=bcol[:, 32:40])
             for q in range(3):
                 w_scale(0, q)
-            for q in range(3):
-                w_cast(1, q)
-            bias_turn()
-            for q in range(3):
-                w_turn(1, q)
             feat_aux_turn(0)
-            wpad_fill(0)
-            x_spread()
+            wpad_fill(slice(0, 2))
             wT_turn(0)
             copies_out()
-            wT_turn(1)
-            copies_out()
+            x_turn()
             for q in range(3):
                 w_quantize(0, q)
             h_quantize(0, 0)
             h_quantize(1, 0)
-            for q in range(3):
-                w_scale(1, q)
             spare_banks.clear()
 
-            cast_in = {}
-            for c in range(2, SETS):
-                for q in range(3):
-                    cast_in.setdefault(2 * c - 7 + (0 if q < N else 1), []).append((c, q))
+            scale_in = {-1: (3, 4), 0: (5, 6), 1: (7, 8), 2: (9, 10), 3: (11, 12), 4: (13, 14), 6: (15, 16), 7: (17, 18), 8: (19, 20), 9: (21, 22), 12: (23,)}
+            load_in = {-1: 4, 1: 5, 2: 6, 4: 7}
 
             def is_unit(i):
                 return 0 <= i < UNITS
 
-            def step(tau, after_empty=None):
-                copies_out()
+            def tiles(tau):
+                return [(t // 3, t % 3) for t in scale_in.get(tau, ())]
+
+            def step(tau, between=None, after_empty=None):
                 if is_unit(tau):
                     z_sigmoid(tau)
-                for c, q in cast_in.get(tau, ()):
-                    if q == R and c + 2 < SETS:
-                        w_load(c + 2)
+                if tau in load_in:
+                    w_load(load_in[tau])
                 if is_unit(tau - 1):
                     h_minus_n(tau - 1, nc.gpsimd)
                 if is_unit(tau + 1):
                     r_empty(tau + 1)
                     z_empty(tau + 1)
+                if after_empty is not None:
+                    after_empty()
                 if is_unit(tau):
                     n_q(tau)
                 if is_unit(tau + 1):
-                    r_sum(tau + 1, nc.gpsimd)
-                for c, q in cast_in.get(tau - 2, ()):
+                    r_sum(tau + 1, nc.vector if tau + 1 == LAST else nc.gpsimd)
+                for c, q in tiles(tau):
                     w_scale(c, q)
-                if after_empty is not None:
-                    after_empty()
                 if is_unit(tau + 2):
                     mm_gi_r(tau + 2)
                     r_helped_copy(tau + 2)
                     mm_gh(tau + 2, R)
                     mm_gh(tau + 2, Z)
+                if between is not None:
+                    between()
                 if is_unit(tau + 1):
                     mm_gh(tau + 1, N)
                 if is_unit(tau):
                     mm_gi_t(tau, N)
                     turn_onto(tau, N, [qq_of[tau]])
                     n_tanh(tau)
-                for c, q in cast_in.get(tau - 1, ()):
-                    w_turn(c, q)
+                if tau % 2 != 0 and 1 <= (tau + 3) // 2 < SETS:
+                    wT_turn((tau + 3) // 2)
+                ahead = tiles(tau + 1)
+                if ahead:
+                    w_turn(*ahead[0])
                 if is_unit(tau + 1):
                     mm_gi_t(tau + 1, Z)
                     turn_onto(tau + 1, Z, [sz_of[tau + 1], cz_of[tau + 1]])
                     r_sigmoid(tau + 1)
+                copies_out()
                 if is_unit(tau + 2):
                     z_side(tau + 2)
-                for c, q in cast_in.get(tau, ()):
+                if len(ahead) > 1:
+                    w_turn(*ahead[1])
+                for c, q in tiles(tau + 3):
                     w_cast(c, q)
                 if is_unit(tau - 1):
                     times_z(tau - 1, nc.gpsimd)
-                    plus_n(tau - 1, nc.vector if tau - 1 in VADD else nc.gpsimd)
-                    store(tau - 1)
-                for c, q in cast_in.get(tau - 2, ()):
+                    if tau - 1 not in VADD:
+                        plus_n(tau - 1, nc.gpsimd)
+                        store(tau - 1)
+                if tau - 2 in VADD:
+                    plus_n(tau - 2, nc.vector)
+                    store(tau - 2)
+                for c, q in tiles(tau):
                     w_quantize(c, q)
-                if tau % 2 == 1 and 2 <= (tau + 5) // 2 < SETS:
-                    wT_turn((tau + 5) // 2)
+
+            def second_half():
+                spare_banks.extend(["tr", "tr", "ghn", "nb", "zb"])
+                for jp in range(2, 4):
+                    for g in range(2):
+                        h_turn(jp, g)
+                feat_aux_turn(1)
+                spare_banks.clear()
 
             def quantize_second_half():
                 h_quantize(0, 1)
                 h_quantize(1, 1)
 
-            step(-3)
-            step(-2)
-            spare_banks.extend(["ghn", "nb", "zb"])
-            for jp in range(2, 4):
-                for g in range(2):
-                    h_turn(jp, g)
-            feat_aux_turn(1)
-            spare_banks.clear()
-            for q in range(3):
-                w_quantize(1, q)
-            step(-1, quantize_second_half)
-            wpad_fill(1)
+            for t in (3, 4, 5, 6):
+                w_cast(t // 3, t % 3)
+            step(-2, second_half)
+            step(-1, None, quantize_second_half)
+            wpad_fill(slice(2, 8))
 
-        for tau in range(0, LAST + 2):
+        for tau in range(0, LAST):
             step(tau)
+
+        i = LAST
+        c, nb = i // 2, i % 2
+        z_sigmoid(i)
+        h_minus_n(i - 1, nc.gpsimd)
+        qq = ew.tile([P, NB], F32, name="qq", tag="qq")
+        nn = ew.tile([P, 4, P], F32, name="nn", tag="nn", bufs=4)
+        dd = stream.tile([P, 4, P], F32, name="dd", tag="dd", bufs=5)
+        for half in range(2):
+            cs = slice(256 * half, 256 * half + 256)
+            nc.vector.scalar_tensor_tensor(
+                out=qq[:, cs], in0=gh_of[(i, N)][:, cs], scalar=bcol[:, 40 + c : 41 + c], in1=gate_of[(i, R)][:, cs], op0=ALU.add, op1=ALU.mult
+            )
+        for half in range(2):
+            mm_gi_t(i, N, half)
+        for half in range(2):
+            turn_onto(i, N, [qq], half)
+            js = slice(2 * half, 2 * half + 2)
+            nc.scalar.activation(out=nn[:, js, :], in_=gi_of[(i, N, half)][:, js, :], func=ACT.Tanh)
+        if i - 2 in VADD:
+            plus_n(i - 2, nc.vector)
+            store(i - 2)
+        times_z(i - 1, nc.gpsimd)
+        hcols = slice(c * P, (c + 1) * P)
+        for half in range(2):
+            js = slice(2 * half, 2 * half + 2)
+            hj = slice(4 * nb + 2 * half, 4 * nb + 2 * half + 2)
+            nc.vector.tensor_tensor(out=dd[:, js, :], in0=h_sb[:, hj, hcols], in1=nn[:, js, :], op=ALU.subtract)
+        for half in range(2):
+            js = slice(2 * half, 2 * half + 2)
+            nc.vector.tensor_tensor(out=dd[:, js, :], in0=gate_of[(i, Z)][:, js, :], in1=dd[:, js, :], op=ALU.mult)
+        plus_n(i - 1, nc.vector)
+        store(i - 1)
+        for half in range(2):
+            js = slice(2 * half, 2 * half + 2)
+            hj = slice(4 * nb + 2 * half, 4 * nb + 2 * half + 2)
+            nc.vector.tensor_tensor(out=dd[:, js, :], in0=nn[:, js, :], in1=dd[:, js, :], op=ALU.add)
+            nc.sync.dma_start(out=outv[:, hj, hcols], in_=dd[:, js, :])

@@ -27,6 +27,8 @@ NAMES = ("r", "z", "n")
 
 
 RH = ()
+SORT = tuple(range(8, 24, 2))
+VC = tuple(range(7, 24, 2))
 ZH = (3, 5, 7, 9, 11, 13, 15)
 VADD = tuple(range(7, 15))
 
@@ -129,7 +131,7 @@ def tile_wavernncell_pa_kernel(tc, x, feat, aux1, h, w_ih, w_hh_bytes, w_hh_scal
 
         def w_cast(c, q):
             wbf = stream.tile([P, H], BF16, name="wbf", tag="wbf", bufs=6)
-            if 3 * c + q < 7:
+            if 3 * c + q < 7 or 3 * c + q in VC:
                 nc.vector.tensor_scalar(
                     out=wbf[:].rearrange("p (u w e) -> p w u e", u=2, e=2),
                     in0=wbytes_of[c][:, q, :].bitcast(FP8).rearrange("p (w u e) -> p w u e", u=2, e=2),
@@ -140,6 +142,11 @@ def tile_wavernncell_pa_kernel(tc, x, feat, aux1, h, w_ih, w_hh_bytes, w_hh_scal
                 sorted_tiles.add((c, q))
             else:
                 nc.scalar.copy(out=wbf[:], in_=wbytes_of[c][:, q, :].bitcast(FP8))
+                if 3 * c + q in SORT:
+                    wbs = stream.tile([P, H], BF16, name="wbs", tag="wbs", bufs=6)
+                    nc.scalar.copy(out=wbs[:].bitcast(F32).rearrange("p (u w) -> p u w", u=2), in_=wbf[:].bitcast(F32).rearrange("p (w u) -> p u w", u=2))
+                    sorted_tiles.add((c, q))
+                    wbf = wbs
             wbf_of[(c, q)] = wbf
 
         def w_turn(c, q):

@@ -26,11 +26,10 @@ R, Z, N = 0, 1, 2
 NAMES = ("r", "z", "n")
 
 
-RH = ()
 SORT = tuple(range(8, 24, 2))
 VC = tuple(range(7, 24, 2))
-ZH = (3, 5, 7, 9, 11, 13, 15)
-VADD = tuple(range(7, 15))
+ZH = tuple(range(8))
+VADD = tuple(range(10, 15))
 
 
 def tile_wavernncell_pa_kernel(tc, x, feat, aux1, h, w_ih, w_hh_bytes, w_hh_scale, b_ih, b_hh, out):
@@ -161,7 +160,7 @@ def tile_wavernncell_pa_kernel(tc, x, feat, aux1, h, w_ih, w_hh_bytes, w_hh_scal
                     nc.tensor.transpose(xt[:, g, u, :], run, ident_f[:])
             xw_of[(c, q)] = xt
 
-        runs = [(0, 2), (2, 1), (3, 2), (5, 2), (7, 2), (9, 2), (11, 4), (15, 4), (19, 4), (23, 1)]
+        runs = [(0, 2), (2, 1)] + [(3 + 2 * k, 2) for k in range(10)] + [(23, 1)]
         run_of = {}
         for k, (first_tile, width) in enumerate(runs):
             for a in range(width):
@@ -202,11 +201,8 @@ def tile_wavernncell_pa_kernel(tc, x, feat, aux1, h, w_ih, w_hh_bytes, w_hh_scal
             wT = wT_of[c]
             ps = acc.tile([P, NB], F32, name="gir", tag="gir")
             gi_of[(i, R)] = ps
-            helped = i in RH
             nc.tensor.matmul(ps[:], lhsT=wT[:, 0, :], rhs=featT[:, cols_of(i)], start=True, stop=False)
-            nc.tensor.matmul(ps[:], lhsT=wT[:, 1, :], rhs=auxT[:, cols_of(i)], start=False, stop=not helped)
-            if helped:
-                nc.tensor.matmul(ps[:], lhsT=wT[:, 7, :], rhs=xs[:, cols_of(i)], start=False, stop=True)
+            nc.tensor.matmul(ps[:], lhsT=wT[:, 1, :], rhs=auxT[:, cols_of(i)], start=False, stop=True)
 
         def mm_gi_t(i, q, half=None):
             c, nb = i // 2, i % 2
@@ -255,31 +251,17 @@ def tile_wavernncell_pa_kernel(tc, x, feat, aux1, h, w_ih, w_hh_bytes, w_hh_scal
             )
             return t
 
-        def r_helped_copy(i):
-            c = i // 2
-            if i in RH:
-                a = ew.tile([P, NB], F32, name="ar", tag="ar")
-                nc.scalar.activation(out=a[:], in_=gi_of[(i, R)][:], func=ACT.Identity, bias=brz[:, c : c + 1], scale=1.0)
-                sum_of[i] = a
-
         def r_empty(i):
-            if i in RH:
-                nc.vector.tensor_tensor(out=sum_of[i][:], in0=sum_of[i][:], in1=gh_of[(i, R)][:], op=ALU.add)
-            else:
-                sum_of[i] = stt(i, R, x0f, 256, gi_of[(i, R)], "ar")
-                sum_of[(i, "h")] = stt(i, R, x1f, 257, gh_of[(i, R)], "cr")
+            sum_of[i] = stt(i, R, x0f, 256, gi_of[(i, R)], "ar")
+            sum_of[(i, "h")] = stt(i, R, x1f, 257, gh_of[(i, R)], "cr")
 
         def r_sum(i, engine):
-            if i not in RH:
-                engine.tensor_tensor(out=sum_of[i][:], in0=sum_of[i][:], in1=sum_of[(i, "h")][:], op=ALU.add)
+            engine.tensor_tensor(out=sum_of[i][:], in0=sum_of[i][:], in1=sum_of[(i, "h")][:], op=ALU.add)
 
         def r_sigmoid(i):
             c = i // 2
             gt = ew.tile([P, NB], F32, name="gr", tag="gr")
-            if i in RH:
-                nc.scalar.activation(out=gt[:], in_=sum_of[i][:], func=ACT.Sigmoid)
-            else:
-                nc.scalar.activation(out=gt[:], in_=sum_of[i][:], func=ACT.Sigmoid, bias=brz[:, c : c + 1], scale=1.0)
+            nc.scalar.activation(out=gt[:], in_=sum_of[i][:], func=ACT.Sigmoid, bias=brz[:, c : c + 1], scale=1.0)
             gate_of[(i, R)] = gt
 
         cz_of = {}
@@ -349,17 +331,17 @@ def tile_wavernncell_pa_kernel(tc, x, feat, aux1, h, w_ih, w_hh_bytes, w_hh_scal
             nc.vector.memset(warm[:], 0.0)
             nc.vector.memset(one[:], 1.0)
             nc.vector.memset(brow[:], 0.0)
-            masks.make_identity(nc, ident_f[:])
             masks.make_identity(nc, ident_b[:])
+            masks.make_identity(nc, ident_f[:])
             nc.vector.memset(wpad[:].rearrange("p a c m -> p (a c m)").bitcast(F32), 0.0)
             nc.vector.memset(xs[64:128, :], 1.0)
 
+            nc.sync.dma_start(out=x_sb[:], in_=x.rearrange("(p j) e -> p j e", j=8))
             w_load(0)
             nc.scalar.dma_start(out=s4[:].rearrange("p g o t -> p (g o) t"), in_=w_hh_scale.rearrange("o (g p t) -> p (o g) t", g=2, p=P, t=4))
             nc.scalar.activation(out=warm[:, 1:2], in_=warm[:, 0:1], func=ACT.Sigmoid)
             nc.sync.dma_start(out=h_sb[:, 0:2, :], in_=hv[:, 0:2, :])
             nc.sync.dma_start(out=h_sb[:, 2:4, :], in_=hv[:, 2:4, :])
-            nc.scalar.dma_start(out=x_sb[:], in_=x.rearrange("(p j) e -> p j e", j=8))
             for k, b in enumerate((b_ih, b_hh)):
                 rows = b.rearrange("(r m) -> r m", m=P)
                 nc.scalar.dma_start(out=brow[24 * k : 24 * k + 16, :], in_=rows[0:16, :])
@@ -404,6 +386,7 @@ def tile_wavernncell_pa_kernel(tc, x, feat, aux1, h, w_ih, w_hh_bytes, w_hh_scal
                 nc.gpsimd.tensor_tensor(out=brz[:], in0=bcol[:, 0:16], in1=bcol[:, 24:40], op=ALU.add)
 
             spare_banks.extend(["tr", "tr", "ghn", "nb", "zb", "ghz", "ghr", "gir"])
+            x_turn()
             for q in range(3):
                 w_cast(0, q)
             for q in range(3):
@@ -420,15 +403,14 @@ def tile_wavernncell_pa_kernel(tc, x, feat, aux1, h, w_ih, w_hh_bytes, w_hh_scal
             wpad_fill(slice(0, 2))
             wT_turn(0)
             copies_out()
-            x_turn()
             for q in range(3):
                 w_quantize(0, q)
             h_quantize(0, 0)
             h_quantize(1, 0)
             spare_banks.clear()
 
-            scale_in = {-1: (3, 4), 0: (5, 6), 1: (7, 8), 2: (9, 10), 3: (11, 12), 4: (13, 14), 6: (15, 16), 7: (17, 18), 8: (19, 20), 9: (21, 22), 12: (23,)}
-            load_in = {-1: 4, 1: 5, 2: 6, 4: 7}
+            scale_in = {-1: (3, 4), 0: (5, 6), 1: (7, 8), 2: (9,), 3: (10,), 4: (11, 12), 5: (13, 14), 6: (15,), 7: (16,), 8: (17, 18), 9: (19, 20), 10: (21,), 11: (22,), 12: (23,)}
+            load_in = {-1: 4, 2: 5, 4: 6, 6: 7}
 
             def is_unit(i):
                 return 0 <= i < UNITS
@@ -439,6 +421,9 @@ def tile_wavernncell_pa_kernel(tc, x, feat, aux1, h, w_ih, w_hh_bytes, w_hh_scal
             def step(tau, between=None, after_empty=None):
                 if is_unit(tau):
                     z_sigmoid(tau)
+                for c, q in tiles(tau + 2):
+                    if (c, q) not in wbf_of and not 3 * c + q in VC:
+                        w_cast(c, q)
                 if tau in load_in:
                     w_load(load_in[tau])
                 if is_unit(tau - 1):
@@ -455,10 +440,14 @@ def tile_wavernncell_pa_kernel(tc, x, feat, aux1, h, w_ih, w_hh_bytes, w_hh_scal
                 for c, q in tiles(tau):
                     w_scale(c, q)
                 if is_unit(tau + 2):
-                    mm_gi_r(tau + 2)
-                    r_helped_copy(tau + 2)
-                    mm_gh(tau + 2, R)
-                    mm_gh(tau + 2, Z)
+                    if tau == -2:
+                        mm_gh(tau + 2, R)
+                        mm_gh(tau + 2, Z)
+                        mm_gi_r(tau + 2)
+                    else:
+                        mm_gi_r(tau + 2)
+                        mm_gh(tau + 2, R)
+                        mm_gh(tau + 2, Z)
                 if between is not None:
                     between()
                 if is_unit(tau + 1):
@@ -482,7 +471,8 @@ def tile_wavernncell_pa_kernel(tc, x, feat, aux1, h, w_ih, w_hh_bytes, w_hh_scal
                 if len(ahead) > 1:
                     w_turn(*ahead[1])
                 for c, q in tiles(tau + 3):
-                    w_cast(c, q)
+                    if 3 * c + q in VC:
+                        w_cast(c, q)
                 if is_unit(tau - 1):
                     times_z(tau - 1, nc.gpsimd)
                     if tau - 1 not in VADD:
@@ -518,7 +508,7 @@ def tile_wavernncell_pa_kernel(tc, x, feat, aux1, h, w_ih, w_hh_bytes, w_hh_scal
         i = LAST
         c, nb = i // 2, i % 2
         z_sigmoid(i)
-        h_minus_n(i - 1, nc.gpsimd)
+        h_minus_n(i - 1, nc.vector)
         qq = ew.tile([P, NB], F32, name="qq", tag="qq")
         nn = ew.tile([P, 4, P], F32, name="nn", tag="nn", bufs=4)
         dd = stream.tile([P, 4, P], F32, name="dd", tag="dd", bufs=5)
@@ -533,10 +523,11 @@ def tile_wavernncell_pa_kernel(tc, x, feat, aux1, h, w_ih, w_hh_bytes, w_hh_scal
             turn_onto(i, N, [qq], half)
             js = slice(2 * half, 2 * half + 2)
             nc.scalar.activation(out=nn[:, js, :], in_=gi_of[(i, N, half)][:, js, :], func=ACT.Tanh)
-        if i - 2 in VADD:
-            plus_n(i - 2, nc.vector)
-            store(i - 2)
-        times_z(i - 1, nc.gpsimd)
+        times_z(i - 1, nc.vector)
+        plus_n(i - 2, nc.gpsimd)
+        store(i - 2)
+        plus_n(i - 1, nc.gpsimd)
+        store(i - 1)
         hcols = slice(c * P, (c + 1) * P)
         for half in range(2):
             js = slice(2 * half, 2 * half + 2)
@@ -545,8 +536,6 @@ def tile_wavernncell_pa_kernel(tc, x, feat, aux1, h, w_ih, w_hh_bytes, w_hh_scal
         for half in range(2):
             js = slice(2 * half, 2 * half + 2)
             nc.vector.tensor_tensor(out=dd[:, js, :], in0=gate_of[(i, Z)][:, js, :], in1=dd[:, js, :], op=ALU.mult)
-        plus_n(i - 1, nc.vector)
-        store(i - 1)
         for half in range(2):
             js = slice(2 * half, 2 * half + 2)
             hj = slice(4 * nb + 2 * half, 4 * nb + 2 * half + 2)

@@ -29,7 +29,7 @@ NAMES = ("r", "z", "n")
 SORT = tuple(range(8, 24, 2))
 VC = tuple(range(7, 24, 2))
 ZH = tuple(range(8))
-VADD = tuple(range(10, 15))
+VADD = tuple(range(5, 15))
 
 
 def tile_wavernncell_pa_kernel(tc, x, feat, aux1, h, w_ih, w_hh_bytes, w_hh_scale, b_ih, b_hh, out):
@@ -48,6 +48,7 @@ def tile_wavernncell_pa_kernel(tc, x, feat, aux1, h, w_ih, w_hh_bytes, w_hh_scal
         outv = out.rearrange("(p j) n -> p j n", j=8)
 
         s4 = keep.tile([P, 2, 1, 4], F32, name="s4")
+        s4w = keep.tile([P, 2, P, 4], F32, name="s4w")
         h_sb = keep.tile([P, 8, H], BF16, name="h_sb")
         wih_sb = [keep.tile([P, SETS, ROW], BF16, name="wih_sb%d" % q) for q in range(3)]
         wpad = keep.tile([P, 2, SETS, P], BF16, name="wpad")
@@ -157,7 +158,7 @@ def tile_wavernncell_pa_kernel(tc, x, feat, aux1, h, w_ih, w_hh_bytes, w_hh_scal
                         run = words[:, 256 * u + P * g : 256 * u + P * (g + 1)]
                     else:
                         run = words[:, 256 * g + u : 256 * (g + 1) : 2]
-                    nc.tensor.transpose(xt[:, g, u, :], run, ident_f[:])
+                    nc.tensor.transpose(xt[:, u, g, :], run, ident_f[:])
             xw_of[(c, q)] = xt
 
         runs = [(0, 2), (2, 1)] + [(3 + 2 * k, 2) for k in range(10)] + [(23, 1)]
@@ -170,13 +171,12 @@ def tile_wavernncell_pa_kernel(tc, x, feat, aux1, h, w_ih, w_hh_bytes, w_hh_scal
             xt = xw_of[(c, q)]
             k, slot = run_of[3 * c + q][0:2]
             wg = wg3[k % 3]
-            for g in range(2):
-                nc.vector.tensor_tensor(
-                    out=wg[:, slot, g * NB : (g + 1) * NB].rearrange("p (m u e) -> p m u e", u=2, e=2),
-                    in0=xt[:, g, :, :].rearrange("p u m -> p (u m)").bitcast(BF16).rearrange("p (u m e) -> p m u e", u=2, e=2),
-                    in1=s4[:, g, :, :].rearrange("p o (u e) -> p o u e", u=2).to_broadcast([P, P, 2, 2]),
-                    op=ALU.mult,
-                )
+            nc.vector.tensor_tensor(
+                out=wg[:, slot, :].rearrange("p (w u e) -> p w u e", u=2, e=2),
+                in0=xt[:].rearrange("p u g m -> p (u g m)").bitcast(BF16).rearrange("p (u w e) -> p w u e", u=2, e=2),
+                in1=s4w[:].rearrange("p g m (u e) -> p (g m) u e", u=2),
+                op=ALU.mult,
+            )
 
         def w_quantize(c, q):
             k, slot, first_tile, width = run_of[3 * c + q]
@@ -386,6 +386,7 @@ def tile_wavernncell_pa_kernel(tc, x, feat, aux1, h, w_ih, w_hh_bytes, w_hh_scal
                 nc.gpsimd.tensor_tensor(out=brz[:], in0=bcol[:, 0:16], in1=bcol[:, 24:40], op=ALU.add)
 
             spare_banks.extend(["tr", "tr", "ghn", "nb", "zb", "ghz", "ghr", "gir"])
+            nc.scalar.copy(out=s4w[:], in_=s4[:].to_broadcast([P, 2, P, 4]))
             x_turn()
             for q in range(3):
                 w_cast(0, q)

@@ -26,9 +26,9 @@ R, Z, N = 0, 1, 2
 NAMES = ("r", "z", "n")
 
 
-SORT = tuple(range(8, 24, 2))
-VC = tuple(range(7, 24, 2))
-ZH = tuple(range(8))
+SORT = tuple(t for t in range(6,24) if t%3>0)
+VC = tuple(t for t in range(6,24) if t%3==0)
+ZH = (1, 3, 5, 7, 9, 11, 13, 15)
 VADD = tuple(range(5, 15))
 
 
@@ -161,7 +161,7 @@ def tile_wavernncell_pa_kernel(tc, x, feat, aux1, h, w_ih, w_hh_bytes, w_hh_scal
                     nc.tensor.transpose(xt[:, u, g, :], run, ident_f[:])
             xw_of[(c, q)] = xt
 
-        runs = [(0, 2), (2, 1)] + [(3 + 2 * k, 2) for k in range(10)] + [(23, 1)]
+        runs = [run for c in range(SETS) for run in ((3 * c, 2), (3 * c + 2, 1))]
         run_of = {}
         for k, (first_tile, width) in enumerate(runs):
             for a in range(width):
@@ -410,8 +410,11 @@ def tile_wavernncell_pa_kernel(tc, x, feat, aux1, h, w_ih, w_hh_bytes, w_hh_scal
             h_quantize(1, 0)
             spare_banks.clear()
 
-            scale_in = {-1: (3, 4), 0: (5, 6), 1: (7, 8), 2: (9,), 3: (10,), 4: (11, 12), 5: (13, 14), 6: (15,), 7: (16,), 8: (17, 18), 9: (19, 20), 10: (21,), 11: (22,), 12: (23,)}
-            load_in = {-1: 4, 2: 5, 4: 6, 6: 7}
+            scale_in = {}
+            for c in range(1, SETS):
+                scale_in[2 * c - 3] = (3 * c + R, 3 * c + Z)
+                scale_in[2 * c - 2] = (3 * c + N,)
+            load_in = {-1: 4, 1: 5, 3: 6, 5: 7}
 
             def is_unit(i):
                 return 0 <= i < UNITS
@@ -457,8 +460,8 @@ def tile_wavernncell_pa_kernel(tc, x, feat, aux1, h, w_ih, w_hh_bytes, w_hh_scal
                     mm_gi_t(tau, N)
                     turn_onto(tau, N, [qq_of[tau]])
                     n_tanh(tau)
-                if tau % 2 != 0 and 1 <= (tau + 3) // 2 < SETS:
-                    wT_turn((tau + 3) // 2)
+                if tau % 2 != 0 and 2 <= (tau + 5) // 2 < SETS:
+                    wT_turn((tau + 5) // 2)
                 ahead = tiles(tau + 1)
                 if ahead:
                     w_turn(*ahead[0])
@@ -466,9 +469,9 @@ def tile_wavernncell_pa_kernel(tc, x, feat, aux1, h, w_ih, w_hh_bytes, w_hh_scal
                     mm_gi_t(tau + 1, Z)
                     turn_onto(tau + 1, Z, [sz_of[tau + 1], cz_of[tau + 1]])
                     r_sigmoid(tau + 1)
-                copies_out()
                 if is_unit(tau + 2):
                     z_side(tau + 2)
+                copies_out()
                 if len(ahead) > 1:
                     w_turn(*ahead[1])
                 for c, q in tiles(tau + 3):
@@ -491,17 +494,18 @@ def tile_wavernncell_pa_kernel(tc, x, feat, aux1, h, w_ih, w_hh_bytes, w_hh_scal
                     for g in range(2):
                         h_turn(jp, g)
                 feat_aux_turn(1)
+                wT_turn(1)
                 spare_banks.clear()
 
             def quantize_second_half():
                 h_quantize(0, 1)
                 h_quantize(1, 1)
 
-            for t in (3, 4, 5, 6):
+            for t in (3, 4, 5):
                 w_cast(t // 3, t % 3)
             step(-2, second_half)
-            step(-1, None, quantize_second_half)
             wpad_fill(slice(2, 8))
+            step(-1, None, quantize_second_half)
 
         for tau in range(0, LAST):
             step(tau)

@@ -29,7 +29,7 @@ NAMES = ("r", "z", "n")
 SORT = tuple(t for t in range(6,24) if t%3>0)
 VC = tuple(t for t in range(6,24) if t%3==0)
 ZH = (1, 3, 5, 7, 9, 11, 13, 15)
-VADD = tuple(range(5, 15))
+VADD = tuple(range(15))
 
 
 def tile_wavernncell_pa_kernel(tc, x, feat, aux1, h, w_ih, w_hh_bytes, w_hh_scale, b_ih, b_hh, out):
@@ -283,6 +283,10 @@ def tile_wavernncell_pa_kernel(tc, x, feat, aux1, h, w_ih, w_hh_bytes, w_hh_scal
             nc.scalar.activation(out=t[:], in_=x1f[:, cols_of(i)], func=ACT.Identity, bias=brz[:, 8 + c : 9 + c], scale=w1z[:, c, :])
             sz_of[i] = t
 
+        def z_join(i):
+            nc.gpsimd.tensor_tensor(out=cz_of[i][:], in0=cz_of[i][:], in1=sz_of[i][:], op=ALU.add)
+            sz_of[i] = None
+
         def z_sigmoid(i):
             gt = ew.tile([P, 4, P], F32, name="gz", tag="gz", bufs=4)
             nc.scalar.activation(out=gt[:], in_=gi_of[(i, Z, None)][:], func=ACT.Sigmoid)
@@ -441,6 +445,8 @@ def tile_wavernncell_pa_kernel(tc, x, feat, aux1, h, w_ih, w_hh_bytes, w_hh_scal
                     n_q(tau)
                 if is_unit(tau + 1):
                     r_sum(tau + 1, nc.vector if tau + 1 == LAST else nc.gpsimd)
+                if is_unit(tau + 1) and tau + 1 not in ZH:
+                    z_join(tau + 1)
                 for c, q in tiles(tau):
                     w_scale(c, q)
                 if is_unit(tau + 2):

@@ -65,7 +65,7 @@ def tile_wavernncell_pa_kernel(tc, x, feat, aux1, h, w_ih, w_hh_bytes, w_hh_scal
         hs = keep.tile([P, 2, B], U8, name="hs", align_bytes=64)
         wq = keep.tile([P, SETS * 3, 256], U32, name="wq", align_bytes=64)
         ws = keep.tile([P, SETS * 3, 256], U8, name="ws", align_bytes=64)
-        wg3 = [keep.tile([P, 4, H], BF16, name="wg%d" % k, align_bytes=64) for k in range(3)]
+        wg3 = [keep.tile([P, 2, H], BF16, name="wg%d" % k, align_bytes=64) for k in range(3)]
         featT = keep.tile([P, B], BF16, name="featT")
         auxT = keep.tile([P, B], BF16, name="auxT")
         xs = keep.tile([P, B], BF16, name="xs")
@@ -369,7 +369,8 @@ def tile_wavernncell_pa_kernel(tc, x, feat, aux1, h, w_ih, w_hh_bytes, w_hh_scal
                         nc.tensor.transpose(px[:, j, :], x_sb[:, j, e : e + 1].to_broadcast([P, P]), ident_b[:])
                     spread = px[:].rearrange("p j b -> p (j b)")
                     nc.scalar.copy(out=xf[:], in_=spread)
-                    nc.scalar.copy(out=xs[32 * e : 32 * e + 32, :], in_=spread[32 * e : 32 * e + 32, :])
+                    rows = slice(32 * e, 32 * e + 32)
+                    nc.gpsimd.tensor_scalar(out=xs[rows, :], in0=xf[rows, :], scalar1=1.0, scalar2=0.0, op0=ALU.mult, op1=ALU.add)
 
             def wpad_fill(cs):
                 for a, q in enumerate((Z, N)):
@@ -392,26 +393,29 @@ def tile_wavernncell_pa_kernel(tc, x, feat, aux1, h, w_ih, w_hh_bytes, w_hh_scal
             spare_banks.extend(["tr", "tr", "ghn", "nb", "zb", "ghz", "ghr", "gir"])
             nc.scalar.copy(out=s4w[:], in_=s4[:].to_broadcast([P, 2, P, 4]))
             x_turn()
-            for q in range(3):
-                w_cast(0, q)
-            for q in range(3):
-                w_turn(0, q)
+            w_cast(0, R)
+            w_cast(0, Z)
+            w_turn(0, R)
+            w_turn(0, Z)
             for jp in range(2):
                 for g in range(2):
                     h_turn(jp, g)
             bias_turn()
             nc.scalar.copy(out=wpad[:, :, :, 64], in_=bcol[:, 8:24].rearrange("p (a c) -> p a c", a=2))
             nc.scalar.copy(out=wpad[:, 0, :, 96], in_=bcol[:, 32:40])
-            for q in range(3):
-                w_scale(0, q)
+            w_scale(0, R)
+            w_scale(0, Z)
+            w_cast(0, N)
+            w_turn(0, N)
             feat_aux_turn(0)
             wpad_fill(slice(0, 2))
             wT_turn(0)
             copies_out()
-            for q in range(3):
-                w_quantize(0, q)
+            w_quantize(0, Z)
             h_quantize(0, 0)
             h_quantize(1, 0)
+            w_scale(0, N)
+            w_quantize(0, N)
             spare_banks.clear()
 
             scale_in = {}
@@ -444,7 +448,7 @@ def tile_wavernncell_pa_kernel(tc, x, feat, aux1, h, w_ih, w_hh_bytes, w_hh_scal
                 if is_unit(tau):
                     n_q(tau)
                 if is_unit(tau + 1):
-                    r_sum(tau + 1, nc.vector if tau + 1 == LAST else nc.gpsimd)
+                    r_sum(tau + 1, nc.vector if tau + 1 >= LAST - 1 else nc.gpsimd)
                 if is_unit(tau + 1) and tau + 1 not in ZH:
                     z_join(tau + 1)
                 for c, q in tiles(tau):
@@ -462,24 +466,28 @@ def tile_wavernncell_pa_kernel(tc, x, feat, aux1, h, w_ih, w_hh_bytes, w_hh_scal
                     between()
                 if is_unit(tau + 1):
                     mm_gh(tau + 1, N)
+                ahead = tiles(tau + 1)
                 if is_unit(tau):
                     mm_gi_t(tau, N)
+                if is_unit(tau):
                     turn_onto(tau, N, [qq_of[tau]])
+                if is_unit(tau + 1):
+                    r_sigmoid(tau + 1)
+                if is_unit(tau):
                     n_tanh(tau)
-                if tau % 2 != 0 and 2 <= (tau + 5) // 2 < SETS:
-                    wT_turn((tau + 5) // 2)
-                ahead = tiles(tau + 1)
-                if ahead:
-                    w_turn(*ahead[0])
                 if is_unit(tau + 1):
                     mm_gi_t(tau + 1, Z)
+                if is_unit(tau + 1):
                     turn_onto(tau + 1, Z, [sz_of[tau + 1], cz_of[tau + 1]])
-                    r_sigmoid(tau + 1)
+                if tau % 2 != 0 and 2 <= (tau + 5) // 2 < SETS:
+                    wT_turn((tau + 5) // 2)
+                if ahead:
+                    w_turn(*ahead[0])
+                if len(ahead) > 1:
+                    w_turn(*ahead[1])
                 if is_unit(tau + 2):
                     z_side(tau + 2)
                 copies_out()
-                if len(ahead) > 1:
-                    w_turn(*ahead[1])
                 for c, q in tiles(tau + 3):
                     if 3 * c + q in VC:
                         w_cast(c, q)

from contextlib import ExitStack

import concourse.masks as masks
import concourse.mybir as mybir

B, H, FEAT, AUX, NS = 1024, 1024, 128, 128, 2
IN = FEAT + AUX + NS
FLOPS = 2 * B * H * 3 * H + 2 * B * IN * 3 * H

F32 = mybir.dt.float32
BF16 = mybir.dt.bfloat16
U32 = mybir.dt.uint32
U8 = mybir.dt.uint8
FP8 = mybir.dt.float8_e4m3fn
FP8X4 = mybir.dt.float8_e4m3fn_x4
ALU = mybir.AluOpType
ACT = mybir.ActivationFunctionType

P = 128
NB = 512
SETS = 8
UNITS = 2 * SETS
LAST = UNITS - 1
ROW = 272
R, Z, N = 0, 1, 2
NAMES = ("r", "z", "n")


SORT = tuple(t for t in range(6,24) if t%3>0)
VC = tuple(t for t in range(6,24) if t%3==0)
ZH = (1, 3, 5, 7, 9, 11, 13, 15)
VADD = tuple(range(15))


def tile_wavernncell_pa_kernel(tc, x, feat, aux1, h, w_ih, w_hh_bytes, w_hh_scale, b_ih, b_hh, out):
    nc = tc.nc

    with ExitStack() as ctx:
        keep = ctx.enter_context(tc.tile_pool(name="keep", bufs=1))
        stream = ctx.enter_context(tc.tile_pool(name="stream", bufs=3))
        ew = ctx.enter_context(tc.tile_pool(name="ew", bufs=2))
        acc = ctx.enter_context(tc.psum_pool(name="acc", bufs=1))
        trp = ctx.enter_context(tc.psum_pool(name="trp", bufs=2))

        hv = h.rearrange("(p j) k -> p j k", j=8)
        wbv = w_hh_bytes.rearrange("(q c m) k -> c m q k", q=3, c=SETS, m=P)
        wihv = w_ih.rearrange("(q c m) f -> q m c f", q=3, c=SETS, m=P)
        outv = out.rearrange("(p j) n -> p j n", j=8)

        s4 = keep.tile([P, 2, 1, 4], F32, name="s4")
        s4w = keep.tile([P, 2, P, 4], F32, name="s4w")
        h_sb = keep.tile([P, 8, H], BF16, name="h_sb")
        wih_sb = [keep.tile([P, SETS, ROW], BF16, name="wih_sb%d" % q) for q in range(3)]
        wpad = keep.tile([P, 2, SETS, P], BF16, name="wpad")
        w1z = keep.tile([P, SETS, 1], F32, name="w1z")
        brow = keep.tile([P, P], BF16, name="brow")
        bcol = keep.tile([P, 48], F32, name="bcol")
        brz = keep.tile([P, 16], F32, name="brz")
        ident_f = keep.tile([P, P], F32, name="ident_f")
        ident_b = keep.tile([P, P], BF16, name="ident_b")
        warm = keep.tile([P, 2], F32, name="warm")
        one = keep.tile([P, 1], F32, name="one")
        hg = keep.tile([P, 2, 4 * B], BF16, name="hg", align_bytes=64)
        hq = keep.tile([P, 2, B], U32, name="hq", align_bytes=64)
        hs = keep.tile([P, 2, B], U8, name="hs", align_bytes=64)
        wq = keep.tile([P, SETS * 3, 256], U32, name="wq", align_bytes=64)
        ws = keep.tile([P, SETS * 3, 256], U8, name="ws", align_bytes=64)
        wg3 = [keep.tile([P, 2, H], BF16, name="wg%d" % k, align_bytes=64) for k in range(3)]
        featT = keep.tile([P, B], BF16, name="featT")
        auxT = keep.tile([P, B], BF16, name="auxT")
        xs = keep.tile([P, B], BF16, name="xs")
        x0f = keep.tile([P, B], BF16, name="x0f")
        x1f = keep.tile([P, B], BF16, name="x1f")

        spare_banks = []
        spare_used = [0]

        def bank(shape, dtype, name):
            if spare_banks:
                tag = spare_banks[spare_used[0] % len(spare_banks)]
                spare_used[0] += 1
                if tag != "tr":
                    return acc.tile(shape, dtype, name=name + tag, tag=tag)
            return trp.tile(shape, dtype, name=name, tag="tr")

        pending = []

        def h_turn(jp, g):
            xt = bank([P, 2, 256], F32, "xt")
            for jj in range(2):
                words = h_sb[:, 2 * jp + jj, :].bitcast(F32)
                for u in range(2):
                    nc.tensor.transpose(xt[:, u, jj * P : (jj + 1) * P], words[:, 256 * g + u : 256 * (g + 1) : 2], ident_f[:])
            dst = hg[:, g, 1024 * jp : 1024 * (jp + 1)].bitcast(F32).rearrange("p (c u) -> p c u", u=2)
            nc.scalar.copy(out=dst, in_=xt[:].rearrange("p u c -> p c u"))

        def h_quantize(g, nb):
            nc.vector.quantize_mx(
                out=hq[:, g, nb * NB : (nb + 1) * NB].bitcast(FP8X4),
                scales=hs[:, g, nb * NB : (nb + 1) * NB],
                in_=hg[:, g, nb * 4 * NB : (nb + 1) * 4 * NB],
            )

        wT_of = {}

        def wT_turn(c):
            pw = bank([P, 8, P], BF16, "pw")
            for q in range(3):
                nc.tensor.transpose(pw[:, 2 * q, :], wih_sb[q][:, c, 0:FEAT], ident_b[:])
                nc.tensor.transpose(pw[:, 2 * q + 1, :], wih_sb[q][:, c, FEAT : FEAT + AUX], ident_b[:])
            nc.tensor.transpose(pw[:, 6, :], wpad[:, 0, c, :], ident_b[:])
            nc.tensor.transpose(pw[:, 7, :], wpad[:, 1, c, :], ident_b[:])
            pending.append((c, pw))

        def copies_out():
            for c, pw in pending:
                wT = stream.tile([P, 8, P], BF16, name="wT", tag="wT", bufs=4)
                nc.scalar.copy(out=wT[:], in_=pw[:])
                wT_of[c] = wT
            pending.clear()

        wbytes_of = {}
        wbf_of = {}
        xw_of = {}
        sorted_tiles = set()

        def w_load(c):
            wbytes = stream.tile([P, 3, H], U8, name="wbytes", tag="wbytes", bufs=4)
            nc.sync.dma_start(out=wbytes[:], in_=wbv[c, :, :, :])
            wbytes_of[c] = wbytes

        def w_cast(c, q):
            wbf = stream.tile([P, H], BF16, name="wbf", tag="wbf", bufs=6)
            if 3 * c + q < 7 or 3 * c + q in VC:
                nc.vector.tensor_scalar(
                    out=wbf[:].rearrange("p (u w e) -> p w u e", u=2, e=2),
                    in0=wbytes_of[c][:, q, :].bitcast(FP8).rearrange("p (w u e) -> p w u e", u=2, e=2),
                    scalar1=one[:],
                    scalar2=None,
                    op0=ALU.mult,
                )
                sorted_tiles.add((c, q))
            else:
                nc.scalar.copy(out=wbf[:], in_=wbytes_of[c][:, q, :].bitcast(FP8))
                if 3 * c + q in SORT:
                    wbs = stream.tile([P, H], BF16, name="wbs", tag="wbs", bufs=6)
                    nc.scalar.copy(out=wbs[:].bitcast(F32).rearrange("p (u w) -> p u w", u=2), in_=wbf[:].bitcast(F32).rearrange("p (w u) -> p u w", u=2))
                    sorted_tiles.add((c, q))
                    wbf = wbs
            wbf_of[(c, q)] = wbf

        def w_turn(c, q):
            words = wbf_of[(c, q)][:].bitcast(F32)
            xt = bank([P, 2, 2, P], F32, "xw")
            for g in range(2):
                for u in range(2):
                    if (c, q) in sorted_tiles:
                        run = words[:, 256 * u + P * g : 256 * u + P * (g + 1)]
                    else:
                        run = words[:, 256 * g + u : 256 * (g + 1) : 2]
                    nc.tensor.transpose(xt[:, u, g, :], run, ident_f[:])
            xw_of[(c, q)] = xt

        runs = [run for c in range(SETS) for run in ((3 * c, 2), (3 * c + 2, 1))]
        run_of = {}
        for k, (first_tile, width) in enumerate(runs):
            for a in range(width):
                run_of[first_tile + a] = (k, a, first_tile, width)

        def w_scale(c, q):
            xt = xw_of[(c, q)]
            k, slot = run_of[3 * c + q][0:2]
            wg = wg3[k % 3]
            nc.vector.tensor_tensor(
                out=wg[:, slot, :].rearrange("p (w u e) -> p w u e", u=2, e=2),
                in0=xt[:].rearrange("p u g m -> p (u g m)").bitcast(BF16).rearrange("p (u w e) -> p w u e", u=2, e=2),
                in1=s4w[:].rearrange("p g m (u e) -> p (g m) u e", u=2),
                op=ALU.mult,
            )

        def w_quantize(c, q):
            k, slot, first_tile, width = run_of[3 * c + q]
            if slot == width - 1:
                nc.vector.quantize_mx(
                    out=wq[:, first_tile : first_tile + width, :].rearrange("p t w -> p (t w)").bitcast(FP8X4),
                    scales=ws[:, first_tile : first_tile + width, :].rearrange("p t w -> p (t w)"),
                    in_=wg3[k % 3][:, 0:width, :].rearrange("p t k -> p (t k)"),
                )

        gi_of = {}
        gh_of = {}
        sum_of = {}
        gate_of = {}

        def cols_of(i):
            nb = i % 2
            return slice(nb * NB, (nb + 1) * NB)

        def mm_gi_r(i):
            c = i // 2
            wT = wT_of[c]
            ps = acc.tile([P, NB], F32, name="gir", tag="gir")
            gi_of[(i, R)] = ps
            nc.tensor.matmul(ps[:], lhsT=wT[:, 0, :], rhs=featT[:, cols_of(i)], start=True, stop=False)
            nc.tensor.matmul(ps[:], lhsT=wT[:, 1, :], rhs=auxT[:, cols_of(i)], start=False, stop=True)

        def mm_gi_t(i, q, half=None):
            c, nb = i // 2, i % 2
            wT = wT_of[c]
            nm = "zb" if q == Z else ("gir" if half == 1 else "nb")
            ps = acc.tile([P, 4, P], F32, name=nm + "t", tag=nm)
            gi_of[(i, q, half)] = ps
            first = 2 if half == 1 else 0
            for j in range(first, 2 if half == 0 else 4):
                blk = slice(nb * NB + j * P, nb * NB + (j + 1) * P)
                nc.tensor.matmul(ps[:, j, :], lhsT=featT[:, blk], rhs=wT[:, 2 * q, :], start=(j == first), stop=False)
                nc.tensor.matmul(ps[:, j, :], lhsT=auxT[:, blk], rhs=wT[:, 2 * q + 1, :], start=False, stop=False)
                if q == N or i in ZH:
                    nc.tensor.matmul(ps[:, j, :], lhsT=xs[:, blk], rhs=wT[:, 7 if q == N else 6, :], start=False, stop=False)

        def turn_onto(i, q, tiles, half=None):
            ps = gi_of[(i, q, half)]
            js = range(2 if half == 1 else 0, 2 if half == 0 else 4)
            tiles = [t for t in tiles if t is not None]
            for a, t in enumerate(tiles):
                for j in js:
                    last = a == len(tiles) - 1 and j == js[-1]
                    nc.tensor.matmul(ps[:, j, :], lhsT=t[:, j * P : (j + 1) * P], rhs=ident_f[:], is_transpose=True, start=False, stop=last)

        def mm_gh(i, q):
            c = i // 2
            nm = "gh" + NAMES[R if q == N and i == LAST else q]
            ps = acc.tile([P, NB], F32, name=nm, tag=nm)
            for g in range(2):
                nc.tensor.matmul_mx(
                    out=ps[:],
                    lhsT=wq[:, 3 * c + q, g * P : (g + 1) * P].bitcast(FP8X4),
                    lhsT_scale=ws[:, 3 * c + q, g * P : (g + 1) * P],
                    rhs=hq[:, g, cols_of(i)].bitcast(FP8X4),
                    rhs_scale=hs[:, g, cols_of(i)],
                    start=(g == 0),
                    stop=(g == 1),
                )
            gh_of[(i, q)] = ps

        def stt(i, q, xf, col, ps, tag):
            t = ew.tile([P, NB], F32, name=tag, tag=tag)
            c = i // 2
            nc.vector.scalar_tensor_tensor(
                out=t[:], in0=xf[:, cols_of(i)], scalar=wih_sb[q][:, c, col : col + 1], in1=ps[:], op0=ALU.mult, op1=ALU.add
            )
            return t

        def r_empty(i):
            sum_of[i] = stt(i, R, x0f, 256, gi_of[(i, R)], "ar")
            sum_of[(i, "h")] = stt(i, R, x1f, 257, gh_of[(i, R)], "cr")

        def r_sum(i, engine):
            engine.tensor_tensor(out=sum_of[i][:], in0=sum_of[i][:], in1=sum_of[(i, "h")][:], op=ALU.add)

        def r_sigmoid(i):
            c = i // 2
            gt = ew.tile([P, NB], F32, name="gr", tag="gr")
            nc.scalar.activation(out=gt[:], in_=sum_of[i][:], func=ACT.Sigmoid, bias=brz[:, c : c + 1], scale=1.0)
            gate_of[(i, R)] = gt

        cz_of = {}
        sz_of = {}

        def z_empty(i):
            if i not in ZH:
                cz_of[i] = stt(i, Z, x0f, 256, gh_of[(i, Z)], "cz")

        def z_side(i):
            c = i // 2
            if i in ZH:
                sz_of[i] = None
                t = ew.tile([P, NB], F32, name="cz", tag="cz")
                nc.scalar.copy(out=t[:], in_=gh_of[(i, Z)][:])
                cz_of[i] = t
                return
            t = ew.tile([P, NB], F32, name="sz", tag="sz")
            nc.scalar.activation(out=t[:], in_=x1f[:, cols_of(i)], func=ACT.Identity, bias=brz[:, 8 + c : 9 + c], scale=w1z[:, c, :])
            sz_of[i] = t

        def z_join(i):
            nc.gpsimd.tensor_tensor(out=cz_of[i][:], in0=cz_of[i][:], in1=sz_of[i][:], op=ALU.add)
            sz_of[i] = None

        def z_sigmoid(i):
            gt = ew.tile([P, 4, P], F32, name="gz", tag="gz", bufs=4)
            nc.scalar.activation(out=gt[:], in_=gi_of[(i, Z, None)][:], func=ACT.Sigmoid)
            gate_of[(i, Z)] = gt

        qq_of = {}

        def n_q(i):
            c = i // 2
            qq = ew.tile([P, NB], F32, name="qq", tag="qq")
            nc.vector.scalar_tensor_tensor(
                out=qq[:], in0=gh_of[(i, N)][:], scalar=bcol[:, 40 + c : 41 + c], in1=gate_of[(i, R)][:], op0=ALU.add, op1=ALU.mult
            )
            qq_of[i] = qq

        def n_tanh(i):
            nn = ew.tile([P, 4, P], F32, name="nn", tag="nn", bufs=4)
            nc.scalar.activation(out=nn[:], in_=gi_of[(i, N, None)][:], func=ACT.Tanh)
            gate_of[(i, N)] = nn

        dd_of = {}

        def h_minus_n(i, engine):
            c, nb = i // 2, i % 2
            dd = stream.tile([P, 4, P], F32, name="dd", tag="dd", bufs=5)
            engine.tensor_tensor(out=dd[:], in0=h_sb[:, 4 * nb : 4 * nb + 4, c * P : (c + 1) * P], in1=gate_of[(i, N)][:], op=ALU.subtract)
            dd_of[i] = dd

        def times_z(i, engine):
            engine.tensor_tensor(out=dd_of[i][:], in0=gate_of[(i, Z)][:], in1=dd_of[i][:], op=ALU.mult)

        def plus_n(i, engine):
            engine.tensor_tensor(out=dd_of[i][:], in0=gate_of[(i, N)][:], in1=dd_of[i][:], op=ALU.add)

        def store(i):
            c, nb = i // 2, i % 2
            nc.sync.dma_start(out=outv[:, 4 * nb : 4 * nb + 4, c * P : (c + 1) * P], in_=dd_of[i][:])

        ctx.enter_context(tc.manual_schedule())

        with tc.tile_pool(name="early", bufs=1) as early:
            x_sb = early.tile([P, 8, NS], BF16, name="x_sb")
            feat_sb = early.tile([P, 8, FEAT], BF16, name="feat_sb")
            aux_sb = early.tile([P, 8, AUX], BF16, name="aux_sb")

            nc.vector.memset(warm[:], 0.0)
            nc.vector.memset(one[:], 1.0)
            nc.vector.memset(brow[:], 0.0)
            masks.make_identity(nc, ident_b[:])
            masks.make_identity(nc, ident_f[:])
            nc.vector.memset(wpad[:].rearrange("p a c m -> p (a c m)").bitcast(F32), 0.0)
            nc.vector.memset(xs[64:128, :], 1.0)

            nc.sync.dma_start(out=x_sb[:], in_=x.rearrange("(p j) e -> p j e", j=8))
            w_load(0)
            nc.scalar.dma_start(out=s4[:].rearrange("p g o t -> p (g o) t"), in_=w_hh_scale.rearrange("o (g p t) -> p (o g) t", g=2, p=P, t=4))
            nc.scalar.activation(out=warm[:, 1:2], in_=warm[:, 0:1], func=ACT.Sigmoid)
            nc.sync.dma_start(out=h_sb[:, 0:2, :], in_=hv[:, 0:2, :])
            nc.sync.dma_start(out=h_sb[:, 2:4, :], in_=hv[:, 2:4, :])
            for k, b in enumerate((b_ih, b_hh)):
                rows = b.rearrange("(r m) -> r m", m=P)
                nc.scalar.dma_start(out=brow[24 * k : 24 * k + 16, :], in_=rows[0:16, :])
                nc.scalar.dma_start(out=brow[24 * k + 16 : 24 * k + 24, :], in_=rows[16:24, :])
            nc.sync.dma_start(out=feat_sb[:].rearrange("p j f -> p (j f)"), in_=feat.rearrange("(p j) f -> p (j f)", j=8))
            nc.sync.dma_start(out=aux_sb[:].rearrange("p j f -> p (j f)"), in_=aux1.rearrange("(p j) f -> p (j f)", j=8))
            for q in range(3):
                nc.sync.dma_start(out=wih_sb[q][:, 0:2, 0:IN], in_=wihv[q, :, 0:2, :])
            w_load(1)
            nc.sync.dma_start(out=h_sb[:, 4:6, :], in_=hv[:, 4:6, :])
            nc.sync.dma_start(out=h_sb[:, 6:8, :], in_=hv[:, 6:8, :])
            w_load(2)
            for q in range(3):
                nc.sync.dma_start(out=wih_sb[q][:, 2:8, 0:IN], in_=wihv[q, :, 2:8, :])
            w_load(3)

            def x_turn():
                for e, xf in enumerate((x0f, x1f)):
                    px = bank([P, 8, P], BF16, "px")
                    for j in range(8):
                        nc.tensor.transpose(px[:, j, :], x_sb[:, j, e : e + 1].to_broadcast([P, P]), ident_b[:])
                    spread = px[:].rearrange("p j b -> p (j b)")
                    nc.scalar.copy(out=xf[:], in_=spread)
                    rows = slice(32 * e, 32 * e + 32)
                    nc.gpsimd.tensor_scalar(out=xs[rows, :], in0=xf[rows, :], scalar1=1.0, scalar2=0.0, op0=ALU.mult, op1=ALU.add)

            def wpad_fill(cs):
                for a, q in enumerate((Z, N)):
                    nc.scalar.copy(out=wpad[:, a, cs, 0:33:32], in_=wih_sb[q][:, cs, 256:258])
                nc.scalar.copy(out=w1z[:, cs, :], in_=wih_sb[Z][:, cs, 257:258])

            def feat_aux_turn(half):
                for src, dst in ((feat_sb, featT), (aux_sb, auxT)):
                    pt = bank([P, 4, P], BF16, "pt")
                    for jj in range(4):
                        nc.tensor.transpose(pt[:, jj, :], src[:, 4 * half + jj, :], ident_b[:])
                    nc.scalar.copy(out=dst[:, half * NB : (half + 1) * NB], in_=pt[:].rearrange("p j b -> p (j b)"))

            def bias_turn():
                pb = bank([P, P], BF16, "pb")
                nc.tensor.transpose(pb[:], brow[:], ident_b[:])
                nc.scalar.copy(out=bcol[:], in_=pb[:, 0:48])
                nc.gpsimd.tensor_tensor(out=brz[:], in0=bcol[:, 0:16], in1=bcol[:, 24:40], op=ALU.add)

            spare_banks.extend(["tr", "tr", "ghn", "nb", "zb", "ghz", "ghr", "gir"])
            nc.scalar.copy(out=s4w[:], in_=s4[:].to_broadcast([P, 2, P, 4]))
            x_turn()
            w_cast(0, R)
            w_cast(0, Z)
            w_turn(0, R)
            w_turn(0, Z)
            for jp in range(2):
                for g in range(2):
                    h_turn(jp, g)
            bias_turn()
            nc.scalar.copy(out=wpad[:, :, :, 64], in_=bcol[:, 8:24].rearrange("p (a c) -> p a c", a=2))
            nc.scalar.copy(out=wpad[:, 0, :, 96], in_=bcol[:, 32:40])
            w_scale(0, R)
            w_scale(0, Z)
            w_cast(0, N)
            w_turn(0, N)
            feat_aux_turn(0)
            wpad_fill(slice(0, 2))
            wT_turn(0)
            copies_out()
            w_quantize(0, Z)
            h_quantize(0, 0)
            h_quantize(1, 0)
            w_scale(0, N)
            w_quantize(0, N)
            spare_banks.clear()

            scale_in = {}
            for c in range(1, SETS):
                scale_in[2 * c - 3] = (3 * c + R, 3 * c + Z)
                scale_in[2 * c - 2] = (3 * c + N,)
            load_in = {-1: 4, 1: 5, 3: 6, 5: 7}

            def is_unit(i):
                return 0 <= i < UNITS

            def tiles(tau):
                return [(t // 3, t % 3) for t in scale_in.get(tau, ())]

            def step(tau, between=None, after_empty=None):
                if is_unit(tau):
                    z_sigmoid(tau)
                for c, q in tiles(tau + 2):
                    if (c, q) not in wbf_of and not 3 * c + q in VC:
                        w_cast(c, q)
                if tau in load_in:
                    w_load(load_in[tau])
                if is_unit(tau - 1):
                    h_minus_n(tau - 1, nc.gpsimd)
                if is_unit(tau + 1):
                    r_empty(tau + 1)
                    z_empty(tau + 1)
                if after_empty is not None:
                    after_empty()
                if is_unit(tau):
                    n_q(tau)
                if is_unit(tau + 1):
                    r_sum(tau + 1, nc.vector if tau + 1 >= LAST - 1 else nc.gpsimd)
                if is_unit(tau + 1) and tau + 1 not in ZH:
                    z_join(tau + 1)
                for c, q in tiles(tau):
                    w_scale(c, q)
                if is_unit(tau + 2):
                    if tau == -2:
                        mm_gh(tau + 2, R)
                        mm_gh(tau + 2, Z)
                        mm_gi_r(tau + 2)
                    else:
                        mm_gi_r(tau + 2)
                        mm_gh(tau + 2, R)
                        mm_gh(tau + 2, Z)
                if between is not None:
                    between()
                if is_unit(tau + 1):
                    mm_gh(tau + 1, N)
                ahead = tiles(tau + 1)
                if is_unit(tau):
                    mm_gi_t(tau, N)
                if is_unit(tau):
                    turn_onto(tau, N, [qq_of[tau]])
                if is_unit(tau + 1):
                    r_sigmoid(tau + 1)
                if is_unit(tau):
                    n_tanh(tau)
                if is_unit(tau + 1):
                    mm_gi_t(tau + 1, Z)
                if is_unit(tau + 1):
                    turn_onto(tau + 1, Z, [sz_of[tau + 1], cz_of[tau + 1]])
                if tau % 2 != 0 and 2 <= (tau + 5) // 2 < SETS:
                    wT_turn((tau + 5) // 2)
                if ahead:
                    w_turn(*ahead[0])
                if len(ahead) > 1:
                    w_turn(*ahead[1])
                if is_unit(tau + 2):
                    z_side(tau + 2)
                copies_out()
                for c, q in tiles(tau + 3):
                    if 3 * c + q in VC:
                        w_cast(c, q)
                if is_unit(tau - 1):
                    times_z(tau - 1, nc.gpsimd)
                    if tau - 1 not in VADD:
                        plus_n(tau - 1, nc.gpsimd)
                        store(tau - 1)
                if tau - 2 in VADD:
                    plus_n(tau - 2, nc.vector)
                    store(tau - 2)
                for c, q in tiles(tau):
                    w_quantize(c, q)

            def second_half():
                spare_banks.extend(["tr", "tr", "ghn", "nb", "zb"])
                for jp in range(2, 4):
                    for g in range(2):
                        h_turn(jp, g)
                feat_aux_turn(1)
                wT_turn(1)
                spare_banks.clear()

            def quantize_second_half():
                h_quantize(0, 1)
                h_quantize(1, 1)

            for t in (3, 4, 5):
                w_cast(t // 3, t % 3)
            step(-2, second_half)
            wpad_fill(slice(2, 8))
            step(-1, None, quantize_second_half)

        for tau in range(0, LAST):
            step(tau)

        i = LAST
        c, nb = i // 2, i % 2
        z_sigmoid(i)
        h_minus_n(i - 1, nc.vector)
        qq = ew.tile([P, NB], F32, name="qq", tag="qq")
        nn = ew.tile([P, 4, P], F32, name="nn", tag="nn", bufs=4)
        dd = stream.tile([P, 4, P], F32, name="dd", tag="dd", bufs=5)
        for half in range(2):
            cs = slice(256 * half, 256 * half + 256)
            nc.vector.scalar_tensor_tensor(
                out=qq[:, cs], in0=gh_of[(i, N)][:, cs], scalar=bcol[:, 40 + c : 41 + c], in1=gate_of[(i, R)][:, cs], op0=ALU.add, op1=ALU.mult
            )
        for half in range(2):
            mm_gi_t(i, N, half)
        for half in range(2):
            turn_onto(i, N, [qq], half)
            js = slice(2 * half, 2 * half + 2)
            nc.scalar.activation(out=nn[:, js, :], in_=gi_of[(i, N, half)][:, js, :], func=ACT.Tanh)
        times_z(i - 1, nc.vector)
        plus_n(i - 2, nc.gpsimd)
        store(i - 2)
        plus_n(i - 1, nc.gpsimd)
        store(i - 1)
        hcols = slice(c * P, (c + 1) * P)
        for half in range(2):
            js = slice(2 * half, 2 * half + 2)
            hj = slice(4 * nb + 2 * half, 4 * nb + 2 * half + 2)
            nc.vector.tensor_tensor(out=dd[:, js, :], in0=h_sb[:, hj, hcols], in1=nn[:, js, :], op=ALU.subtract)
        for half in range(2):
            js = slice(2 * half, 2 * half + 2)
            nc.vector.tensor_tensor(out=dd[:, js, :], in0=gate_of[(i, Z)][:, js, :], in1=dd[:, js, :], op=ALU.mult)
        for half in range(2):
            js = slice(2 * half, 2 * half + 2)
            hj = slice(4 * nb + 2 * half, 4 * nb + 2 * half + 2)
            nc.vector.tensor_tensor(out=dd[:, js, :], in0=nn[:, js, :], in1=dd[:, js, :], op=ALU.add)
            nc.sync.dma_start(out=outv[:, hj, hcols], in_=dd[:, js, :])
